import numpy as np
import ml_dtypes


def mxq(x, axis, fmt="e4m3"):
    dtype, down = {"e4m3": (ml_dtypes.float8_e4m3fn, 7), "e5m2": (ml_dtypes.float8_e5m2, 14)}[fmt]
    v = np.moveaxis(np.asarray(x, np.float32).astype(ml_dtypes.bfloat16).astype(np.float64), axis, -1)
    blocks = v.reshape(v.shape[:-1] + (-1, 32))
    amax = np.abs(blocks).max(-1, keepdims=True)
    byte = np.maximum(np.where(amax > 0, np.frexp(amax)[1] - 1 + 127, 0) - down, 1)
    scale = np.exp2(byte - 127.0)
    codes = (blocks / scale).astype(np.float32).astype(dtype).astype(np.float64)
    return np.moveaxis((codes * scale).reshape(v.shape), -1, axis)


WIDE = False


def mx_kscale(k):
    if not WIDE:
        return np.ones(k)
    levels = np.array([10, -10, 5, -5, 0])
    a = np.random.permutation(np.resize(levels, k // 512 * 4)).reshape(k // 512, 4)
    idx = np.arange(k)
    return np.exp2(a[idx // 512, idx % 128 // 32])


BF16 = ml_dtypes.bfloat16


def bf(x):
    return np.asarray(x, np.float32).astype(BF16)


def f64(x):
    return np.asarray(x).astype(np.float64)


B, DS, HH, WW, HID, HL, REP, GRP = 4, 64, 64, 64, 128, 1024, 8, 4
C = 2 * DS
CN = REP * C


def elu(v):
    return np.where(v > 0.0, v, np.exp(np.minimum(v, 0.0)) - 1.0)


def neighbor_sum(x):
    xp = np.pad(x, ((0, 0), (0, 0), (1, 1), (1, 1)))
    full = sum(xp[:, :, di:di + HH, dj:dj + WW] for di in range(3) for dj in range(3))
    return full - x


def to_rows(t):
    return t.transpose(0, 2, 3, 1).reshape(B * HH * WW, t.shape[1])


def to_maps(r):
    return r.reshape(B, HH, WW, r.shape[1]).transpose(0, 3, 1, 2)


def setup_inputs():
    sc = mx_kscale(CN)[::REP]
    return {"x_cat": bf(np.random.standard_normal((B, C, HH, WW)) * 0.4 * sc[None, :, None, None]),
            "w1": bf(np.random.standard_normal((HID, CN)) / np.sqrt(CN) / np.repeat(sc, REP)[None, :])}


def reference(x_cat, w1):
    nbr = neighbor_sum(f64(x_cat))
    xn = np.repeat(nbr, REP, axis=1)
    z = mxq(to_rows(xn), 1, "e4m3") @ mxq(f64(w1), 1, "e4m3").T
    return to_maps(elu(z))

@@ -1,0 +1,207 @@
+from contextlib import ExitStack
+
+import concourse.mybir as mybir
+from concourse.masks import make_identity
+
+FP8X4 = mybir.dt.float8_e4m3fn_x4
+BF16 = mybir.dt.bfloat16
+F32 = mybir.dt.float32
+U32 = mybir.dt.uint32
+U8 = mybir.dt.uint8
+ADD = mybir.AluOpType.add
+MULT = mybir.AluOpType.mult
+MAX = mybir.AluOpType.max
+ACT = mybir.ActivationFunctionType
+
+P = 128
+B = 4
+HH = 64
+WW = 64
+PIX = HH * WW
+PITCH = 68
+ROWS = 16
+NPX = ROWS * WW
+NT = 512
+
+FLOPS = 2 * B * PIX * 1024 * P
+
+
+def tile_qca_operator_deep_pa_t_kernel(tc, x_cat, w1, out):
+    nc = tc.nc
+    with ExitStack() as ctx:
+        const = ctx.enter_context(tc.tile_pool(name="const", bufs=1))
+        work = ctx.enter_context(tc.tile_pool(name="work", bufs=3))
+        psw = ctx.enter_context(tc.psum_pool(name="psw", bufs=1))
+        psum = ctx.enter_context(tc.psum_pool(name="psum", bufs=6))
+        ctx.enter_context(tc.manual_schedule())
+
+        xz = [const.tile([P, (HH + 2) * WW], BF16, name="xz%d" % b) for b in range(B)]
+        for b in range(B):
+            nc.vector.memset(xz[b][:, 0:WW], 0.0)
+            nc.vector.memset(xz[b][:, (HH + 1) * WW : (HH + 2) * WW], 0.0)
+
+        def load_rows(b, r0, r1):
+            xv = x_cat[b].rearrange("(h a j i) y x -> h a i j (y x)", h=2, a=2, j=8, i=4)
+            for h in range(2):
+                for a in range(2):
+                    for i in range(4):
+                        p0 = 64 * h + 4 * a + i
+                        nc.sync.dma_start(
+                            out=xz[b][p0 : 64 * h + 64 : 8, (r0 + 1) * WW : (r1 + 1) * WW],
+                            in_=xv[h, a, i][:, r0 * WW : r1 * WW],
+                        )
+
+        w_sb = const.tile([P, 1024], BF16, name="w_sb")
+        nc.scalar.dma_start(out=w_sb, in_=w1)
+        load_rows(0, 0, ROWS + 1)
+        load_rows(0, ROWS + 1, HH)
+        for b in range(1, B):
+            load_rows(b, 0, HH)
+
+        ident = const.tile([P, P], BF16, name="ident")
+        make_identity(nc, ident)
+        ones = const.tile([P, 1], F32, name="ones")
+        nc.vector.memset(ones, 1.0)
+        vcs = [const.tile([P, ROWS * PITCH + 8], F32, name="vc%d" % k) for k in range(3)]
+        for k in range(3):
+            nc.gpsimd.memset(vcs[k], 0.0)
+
+        w_q = const.tile([P, 8, P], BF16, name="w_q")
+        for h in range(2):
+            for a in range(2):
+                nc.vector.tensor_copy(
+                    out=w_q[:, :, 64 * h : 64 * h + 64].rearrange(
+                        "o r (j a i) -> o r j a i", j=8, a=2, i=4
+                    )[:, :, :, a, :],
+                    in_=w_sb[:, (2 * h + a) * 256 : (2 * h + a + 1) * 256].rearrange(
+                        "o (j i r) -> o r j i", j=8, i=4, r=8
+                    ),
+                )
+        w_t = psw.tile([P, 8, P], BF16, name="w_t")
+        for r in range(8):
+            nc.tensor.transpose(w_t[:, r, :], w_q[:, r, :], ident)
+        w_g = const.tile([P, 2, P, 4], BF16, name="w_g", align_bytes=64)
+        nc.scalar.copy(out=w_g, in_=w_t.rearrange("p (g t) o -> p g o t", g=2, t=4))
+        w_codes = const.tile([P, 2 * P], U32, name="w_codes", align_bytes=64)
+        w_scl = const.tile([P, 2 * P], U8, name="w_scl", align_bytes=64)
+
+        def quantise_w():
+            nc.vector.quantize_mx(
+                out=w_codes.bitcast(FP8X4),
+                scales=w_scl,
+                in_=w_g.rearrange("p g o t -> p (g o t)"),
+            )
+
+        def padded(t, off, rows):
+            return t[:, off : off + rows * PITCH].rearrange("p (r c) -> p r c", c=PITCH)[:, :, 0:WW]
+
+        def rowsof(ap):
+            return ap.rearrange("p (r c) -> p r c", c=WW)
+
+        chunks = []
+        for b in range(B):
+            sizes = [16, 16, 16, 16] if b < B - 1 else [16, 16, 16, 8, 4, 4]
+            y0 = 0
+            for rows in sizes:
+                chunks.append((b, y0, rows))
+                y0 += rows
+        st = [dict() for c in chunks]
+
+        def adds(i):
+            b, y0, rows = chunks[i]
+            n = rows * WW
+            vc = vcs[i % 3]
+            up = xz[b][:, y0 * WW : y0 * WW + n]
+            mid = xz[b][:, (y0 + 1) * WW : (y0 + 1) * WW + n]
+            dn = xz[b][:, (y0 + 2) * WW : (y0 + 2) * WW + n]
+            vo = work.tile([P, NPX], F32, name="vo")
+            nc.vector.tensor_tensor(out=vo[:, :n], in0=up, in1=dn, op=ADD)
+            nc.vector.tensor_tensor(out=padded(vc, 4, rows), in0=rowsof(vo[:, :n]), in1=rowsof(mid), op=ADD)
+            rr = work.tile([P, NPX], F32, name="rr")
+            nc.vector.tensor_tensor(
+                out=rowsof(rr[:, :n]), in0=padded(vc, 3, rows), in1=padded(vc, 5, rows), op=ADD
+            )
+            nc.vector.tensor_tensor(out=rr[:, :n], in0=rr[:, :n], in1=vo[:, :n], op=ADD)
+            st[i]["rr"] = rr
+
+        def repeat(i):
+            n = chunks[i][2] * WW
+            rep = work.tile([P, 4 * NPX], BF16, name="rep", align_bytes=64)
+            nc.scalar.copy(
+                out=rep[:, : 4 * n].rearrange("p (n t) -> p n t", t=4),
+                in_=st[i]["rr"][:, :n].unsqueeze(2).to_broadcast([P, n, 4]),
+            )
+            st[i]["rep"] = rep
+
+        def quantise(i):
+            n = chunks[i][2] * WW
+            codes = work.tile([P, 2, NPX], U32, name="codes", align_bytes=64)
+            scl = work.tile([P, 2, NPX], U8, name="scl", align_bytes=64)
+            for g in range(2):
+                nc.vector.quantize_mx(
+                    out=codes[:, g, :n].bitcast(FP8X4), scales=scl[:, g, :n], in_=st[i]["rep"][:, : 4 * n]
+                )
+            st[i]["codes"] = codes
+            st[i]["scl"] = scl
+
+        def multiply(i):
+            n = chunks[i][2] * WW
+            codes = st[i]["codes"]
+            scl = st[i]["scl"]
+            accs = []
+            for c0 in range(0, n, NT):
+                w = min(NT, n - c0)
+                acc = psum.tile([P, NT], F32, name="acc")
+                accs.append(acc)
+                for g in range(2):
+                    nc.tensor.matmul_mx(
+                        out=acc[:, :w],
+                        lhsT=w_codes[:, g * P : (g + 1) * P].bitcast(FP8X4),
+                        lhsT_scale=w_scl[:, g * P : (g + 1) * P],
+                        rhs=codes[:, g, c0 : c0 + w].bitcast(FP8X4),
+                        rhs_scale=scl[:, g, c0 : c0 + w],
+                        start=(g == 0),
+                        stop=(g == 1),
+                    )
+            st[i]["accs"] = accs
+
+        def exps(i):
+            n = chunks[i][2] * WW
+            ee = work.tile([P, NPX], F32, name="ee")
+            for k, c0 in enumerate(range(0, n, NT)):
+                w = min(NT, n - c0)
+                nc.scalar.activation(out=ee[:, c0 : c0 + w], in_=st[i]["accs"][k][:, :w], func=ACT.Exp)
+            nc.scalar.activation(out=ee[:, :n], in_=ee[:, :n], func=ACT.Relu, bias=ones, scale=-1.0)
+            st[i]["ee"] = ee
+
+        def finish(i):
+            b, y0, rows = chunks[i]
+            n = rows * WW
+            oo = work.tile([P, NPX], F32, name="oo")
+            for k, c0 in enumerate(range(0, n, NT)):
+                w = min(NT, n - c0)
+                nc.vector.scalar_tensor_tensor(
+                    out=oo[:, c0 : c0 + w],
+                    in0=st[i]["ee"][:, c0 : c0 + w],
+                    scalar=-1.0,
+                    in1=st[i]["accs"][k][:, :w],
+                    op0=MULT,
+                    op1=MAX,
+                )
+            nc.sync.dma_start(
+                out=out[b].rearrange("o y x -> o (y x)")[:, y0 * WW : y0 * WW + n], in_=oo[:, :n]
+            )
+
+        nch = len(chunks)
+        for i in range(nch + 2):
+            if i < nch:
+                adds(i)
+                repeat(i)
+            if i == 1:
+                quantise_w()
+            if 1 <= i <= nch:
+                quantise(i - 1)
+                multiply(i - 1)
+                exps(i - 1)
+            if i >= 2:
+                finish(i - 2)

@@ -22,6 +22,9 @@ PITCH = 68
 ROWS = 16
 NPX = ROWS * WW
 NT = 512
+PE_ROWS = 8
+LAG_Q = 2
+LAG_F = 3
 
 FLOPS = 2 * B * PIX * 1024 * P
 
@@ -32,7 +35,8 @@ def tile_qca_operator_deep_pa_t_kernel(tc, x_cat, w1, out):
         const = ctx.enter_context(tc.tile_pool(name="const", bufs=1))
         work = ctx.enter_context(tc.tile_pool(name="work", bufs=3))
         psw = ctx.enter_context(tc.psum_pool(name="psw", bufs=1))
-        psum = ctx.enter_context(tc.psum_pool(name="psum", bufs=6))
+        psum = ctx.enter_context(tc.psum_pool(name="psum", bufs=5))
+        psn = ctx.enter_context(tc.psum_pool(name="psn", bufs=2))
         ctx.enter_context(tc.manual_schedule())
 
         xz = [const.tile([P, (HH + 2) * WW], BF16, name="xz%d" % b) for b in range(B)]
@@ -40,26 +44,28 @@ def tile_qca_operator_deep_pa_t_kernel(tc, x_cat, w1, out):
             nc.vector.memset(xz[b][:, 0:WW], 0.0)
             nc.vector.memset(xz[b][:, (HH + 1) * WW : (HH + 2) * WW], 0.0)
 
-        def load_rows(b, r0, r1):
+        def load_rows(b, r0, r1, queues):
             xv = x_cat[b].rearrange("(h a j i) y x -> h a i j (y x)", h=2, a=2, j=8, i=4)
             for h in range(2):
                 for a in range(2):
                     for i in range(4):
                         p0 = 64 * h + 4 * a + i
-                        nc.sync.dma_start(
+                        queues[i % len(queues)].dma_start(
                             out=xz[b][p0 : 64 * h + 64 : 8, (r0 + 1) * WW : (r1 + 1) * WW],
                             in_=xv[h, a, i][:, r0 * WW : r1 * WW],
                         )
 
         w_sb = const.tile([P, 1024], BF16, name="w_sb")
-        nc.scalar.dma_start(out=w_sb, in_=w1)
-        load_rows(0, 0, ROWS + 1)
-        load_rows(0, ROWS + 1, HH)
+        nc.gpsimd.dma_start(out=w_sb, in_=w1)
+        load_rows(0, 0, ROWS + 1, [nc.sync, nc.scalar])
+        load_rows(0, ROWS + 1, HH, [nc.sync])
         for b in range(1, B):
-            load_rows(b, 0, HH)
+            load_rows(b, 0, HH, [nc.sync])
 
         ident = const.tile([P, P], BF16, name="ident")
         make_identity(nc, ident)
+        identf = const.tile([P, P], F32, name="identf")
+        make_identity(nc, identf)
         ones = const.tile([P, 1], F32, name="ones")
         nc.vector.memset(ones, 1.0)
         vcs = [const.tile([P, ROWS * PITCH + 8], F32, name="vc%d" % k) for k in range(3)]
@@ -107,50 +113,94 @@ def tile_qca_operator_deep_pa_t_kernel(tc, x_cat, w1, out):
                 y0 += rows
         st = [dict() for c in chunks]
 
-        def adds(i):
-            b, y0, rows = chunks[i]
+        def add_ops(i):
+            rows = chunks[i][2]
+            st[i]["vo"] = work.tile([P, NPX], F32, name="vo")
+            st[i]["rr"] = work.tile([P, NPX], F32, name="rr")
+            if i >= LAG_Q:
+                return add_chain(i, 0, rows, rows - PE_ROWS if offloaded(i) else rows)
+            half = rows // 2
+            pairs = zip(add_chain(i, 0, half, half), add_chain(i, half, half, half))
+            return [op for pair in pairs for op in pair]
+
+        def add_chain(i, ra, rows, rv):
+            b, y0, all_rows = chunks[i]
+            ya = y0 + ra
             n = rows * WW
             vc = vcs[i % 3]
-            up = xz[b][:, y0 * WW : y0 * WW + n]
-            mid = xz[b][:, (y0 + 1) * WW : (y0 + 1) * WW + n]
-            dn = xz[b][:, (y0 + 2) * WW : (y0 + 2) * WW + n]
-            vo = work.tile([P, NPX], F32, name="vo")
-            nc.vector.tensor_tensor(out=vo[:, :n], in0=up, in1=dn, op=ADD)
-            nc.vector.tensor_tensor(out=padded(vc, 4, rows), in0=rowsof(vo[:, :n]), in1=rowsof(mid), op=ADD)
-            rr = work.tile([P, NPX], F32, name="rr")
-            nc.vector.tensor_tensor(
-                out=rowsof(rr[:, :n]), in0=padded(vc, 3, rows), in1=padded(vc, 5, rows), op=ADD
-            )
-            nc.vector.tensor_tensor(out=rr[:, :n], in0=rr[:, :n], in1=vo[:, :n], op=ADD)
-            st[i]["rr"] = rr
+            up = xz[b][:, ya * WW : ya * WW + n]
+            mid = xz[b][:, (ya + 1) * WW : (ya + 1) * WW + n]
+            dn = xz[b][:, (ya + 2) * WW : (ya + 2) * WW + n]
+            vo = st[i]["vo"][:, ra * WW : ra * WW + n]
+            vov = st[i]["vo"][:, ra * WW : (ra + rv) * WW]
+            rr = st[i]["rr"][:, ra * WW : (ra + rv) * WW]
+            off = ra * PITCH
+            return [
+                lambda: nc.vector.tensor_tensor(out=vo, in0=up, in1=dn, op=ADD),
+                lambda: nc.vector.tensor_tensor(
+                    out=padded(vc, off + 4, rows), in0=rowsof(vo), in1=rowsof(mid), op=ADD
+                ),
+                lambda: nc.vector.tensor_tensor(
+                    out=rowsof(rr), in0=padded(vc, off + 3, rv), in1=padded(vc, off + 5, rv), op=ADD
+                ),
+                lambda: nc.vector.tensor_tensor(out=rr, in0=rr, in1=vov, op=ADD),
+            ]
+
+        def offloaded(i):
+            return i in (2, 4, 6, 8, 10, 12, 13, 14)
+
+        def pe_adds(i):
+            rows = chunks[i][2]
+            rv = rows - PE_ROWS
+            vc = vcs[i % 3]
+            accn = psn.tile([P, NT], F32, name="accn")
+            st[i]["accn"] = accn
+            terms = [
+                padded(vc, 3 + rv * PITCH, PE_ROWS),
+                padded(vc, 5 + rv * PITCH, PE_ROWS),
+                rowsof(st[i]["vo"][:, rv * WW : rows * WW]),
+            ]
+            for k, term in enumerate(terms):
+                nc.tensor.matmul(out=rowsof(accn), lhsT=identf, rhs=term, start=(k == 0), stop=(k == 2))
 
         def repeat(i):
             n = chunks[i][2] * WW
             rep = work.tile([P, 4 * NPX], BF16, name="rep", align_bytes=64)
+            nv = n - NT if offloaded(i) else n
             nc.scalar.copy(
-                out=rep[:, : 4 * n].rearrange("p (n t) -> p n t", t=4),
-                in_=st[i]["rr"][:, :n].unsqueeze(2).to_broadcast([P, n, 4]),
+                out=rep[:, : 4 * nv].rearrange("p (n t) -> p n t", t=4),
+                in_=st[i]["rr"][:, :nv].unsqueeze(2).to_broadcast([P, nv, 4]),
             )
+            if offloaded(i):
+                nc.scalar.copy(
+                    out=rep[:, 4 * nv : 4 * n].rearrange("p (n t) -> p n t", t=4),
+                    in_=st[i]["accn"].unsqueeze(2).to_broadcast([P, NT, 4]),
+                )
             st[i]["rep"] = rep
 
-        def quantise(i):
+        def quant_ops(i):
             n = chunks[i][2] * WW
             codes = work.tile([P, 2, NPX], U32, name="codes", align_bytes=64)
             scl = work.tile([P, 2, NPX], U8, name="scl", align_bytes=64)
-            for g in range(2):
-                nc.vector.quantize_mx(
-                    out=codes[:, g, :n].bitcast(FP8X4), scales=scl[:, g, :n], in_=st[i]["rep"][:, : 4 * n]
-                )
             st[i]["codes"] = codes
             st[i]["scl"] = scl
 
-        def multiply(i):
+            def one(g):
+                return lambda: nc.vector.quantize_mx(
+                    out=codes[:, g, :n].bitcast(FP8X4), scales=scl[:, g, :n], in_=st[i]["rep"][:, : 4 * n]
+                )
+
+            return [one(0), one(1)]
+
+        def spans(i):
             n = chunks[i][2] * WW
+            return [(c0, min(NT, n - c0)) for c0 in range(0, n, NT)]
+
+        def multiply(i):
             codes = st[i]["codes"]
             scl = st[i]["scl"]
             accs = []
-            for c0 in range(0, n, NT):
-                w = min(NT, n - c0)
+            for c0, w in spans(i):
                 acc = psum.tile([P, NT], F32, name="acc")
                 accs.append(acc)
                 for g in range(2):
@@ -166,21 +216,21 @@ def tile_qca_operator_deep_pa_t_kernel(tc, x_cat, w1, out):
             st[i]["accs"] = accs
 
         def exps(i):
-            n = chunks[i][2] * WW
             ee = work.tile([P, NPX], F32, name="ee")
-            for k, c0 in enumerate(range(0, n, NT)):
-                w = min(NT, n - c0)
+            for k, (c0, w) in enumerate(spans(i)):
                 nc.scalar.activation(out=ee[:, c0 : c0 + w], in_=st[i]["accs"][k][:, :w], func=ACT.Exp)
-            nc.scalar.activation(out=ee[:, :n], in_=ee[:, :n], func=ACT.Relu, bias=ones, scale=-1.0)
+            for c0, w in spans(i):
+                nc.scalar.activation(
+                    out=ee[:, c0 : c0 + w], in_=ee[:, c0 : c0 + w], func=ACT.Relu, bias=ones, scale=-1.0
+                )
             st[i]["ee"] = ee
 
-        def finish(i):
-            b, y0, rows = chunks[i]
-            n = rows * WW
+        def finish_ops(i):
             oo = work.tile([P, NPX], F32, name="oo")
-            for k, c0 in enumerate(range(0, n, NT)):
-                w = min(NT, n - c0)
-                nc.vector.scalar_tensor_tensor(
+            st[i]["oo"] = oo
+
+            def one(k, c0, w):
+                return lambda: nc.vector.scalar_tensor_tensor(
                     out=oo[:, c0 : c0 + w],
                     in0=st[i]["ee"][:, c0 : c0 + w],
                     scalar=-1.0,
@@ -188,20 +238,35 @@ def tile_qca_operator_deep_pa_t_kernel(tc, x_cat, w1, out):
                     op0=MULT,
                     op1=MAX,
                 )
+
+            return [one(k, c0, w) for k, (c0, w) in enumerate(spans(i))]
+
+        def store(i):
+            b, y0, rows = chunks[i]
+            n = rows * WW
             nc.sync.dma_start(
-                out=out[b].rearrange("o y x -> o (y x)")[:, y0 * WW : y0 * WW + n], in_=oo[:, :n]
+                out=out[b].rearrange("o y x -> o (y x)")[:, y0 * WW : y0 * WW + n], in_=st[i]["oo"][:, :n]
             )
 
         nch = len(chunks)
-        for i in range(nch + 2):
-            if i < nch:
-                adds(i)
-                repeat(i)
-            if i == 1:
+        for i in range(nch + LAG_F):
+            a_ops = add_ops(i) if i < nch else []
+            q_ops = quant_ops(i - LAG_Q) if 0 <= i - LAG_Q < nch else []
+            f_ops = finish_ops(i - LAG_F) if 0 <= i - LAG_F < nch else []
+            if i == LAG_Q:
                 quantise_w()
-            if 1 <= i <= nch:
-                quantise(i - 1)
-                multiply(i - 1)
-                exps(i - 1)
-            if i >= 2:
-                finish(i - 2)
+            others = q_ops + f_ops
+            for k in range(max(len(a_ops), len(others))):
+                if k < len(a_ops):
+                    a_ops[k]()
+                if k < len(others):
+                    others[k]()
+                if q_ops and k == len(q_ops) - 1:
+                    multiply(i - LAG_Q)
+                    exps(i - LAG_Q)
+                if a_ops and k == 1 and offloaded(i):
+                    pe_adds(i)
+            if a_ops:
+                repeat(i)
+            if f_ops:
+                store(i - LAG_F)

@@ -9,8 +9,7 @@ F32 = mybir.dt.float32
 U32 = mybir.dt.uint32
 U8 = mybir.dt.uint8
 ADD = mybir.AluOpType.add
-MULT = mybir.AluOpType.mult
-MAX = mybir.AluOpType.max
+MIN = mybir.AluOpType.min
 ACT = mybir.ActivationFunctionType
 
 P = 128
@@ -66,8 +65,6 @@ def tile_qca_operator_deep_pa_t_kernel(tc, x_cat, w1, out):
         make_identity(nc, ident)
         identf = const.tile([P, P], F32, name="identf")
         make_identity(nc, identf)
-        ones = const.tile([P, 1], F32, name="ones")
-        nc.vector.memset(ones, 1.0)
         vcs = [const.tile([P, ROWS * PITCH + 8], F32, name="vc%d" % k) for k in range(3)]
         for k in range(3):
             nc.gpsimd.memset(vcs[k], 0.0)
@@ -75,7 +72,7 @@ def tile_qca_operator_deep_pa_t_kernel(tc, x_cat, w1, out):
         w_q = const.tile([P, 8, P], BF16, name="w_q")
         for h in range(2):
             for a in range(2):
-                nc.vector.tensor_copy(
+                nc.scalar.copy(
                     out=w_q[:, :, 64 * h : 64 * h + 64].rearrange(
                         "o r (j a i) -> o r j a i", j=8, a=2, i=4
                     )[:, :, :, a, :],
@@ -217,29 +214,27 @@ def tile_qca_operator_deep_pa_t_kernel(tc, x_cat, w1, out):
 
         def exps(i):
             ee = work.tile([P, NPX], F32, name="ee")
+            oo = work.tile([P, NPX], F32, name="oo")
             for k, (c0, w) in enumerate(spans(i)):
                 nc.scalar.activation(out=ee[:, c0 : c0 + w], in_=st[i]["accs"][k][:, :w], func=ACT.Exp)
-            for c0, w in spans(i):
-                nc.scalar.activation(
-                    out=ee[:, c0 : c0 + w], in_=ee[:, c0 : c0 + w], func=ACT.Relu, bias=ones, scale=-1.0
-                )
+                nc.scalar.activation(out=oo[:, c0 : c0 + w], in_=st[i]["accs"][k][:, :w], func=ACT.Relu)
             st[i]["ee"] = ee
-
-        def finish_ops(i):
-            oo = work.tile([P, NPX], F32, name="oo")
             st[i]["oo"] = oo
 
-            def one(k, c0, w):
+        def finish_ops(i):
+            oo = st[i]["oo"]
+
+            def one(c0, w):
                 return lambda: nc.vector.scalar_tensor_tensor(
                     out=oo[:, c0 : c0 + w],
                     in0=st[i]["ee"][:, c0 : c0 + w],
                     scalar=-1.0,
-                    in1=st[i]["accs"][k][:, :w],
-                    op0=MULT,
-                    op1=MAX,
+                    in1=oo[:, c0 : c0 + w],
+                    op0=ADD,
+                    op1=MIN,
                 )
 
-            return [one(k, c0, w) for k, (c0, w) in enumerate(spans(i))]
+            return [one(c0, w) for c0, w in spans(i)]
 
         def store(i):
             b, y0, rows = chunks[i]

@@ -21,7 +21,7 @@ PITCH = 68
 ROWS = 16
 NPX = ROWS * WW
 NT = 512
-PE_ROWS = 8
+PE_ROWS = {2: 8, 3: 4, 4: 8, 6: 8, 8: 8, 10: 8, 12: 8, 13: 8, 14: 8}
 LAG_Q = 2
 LAG_F = 3
 
@@ -57,7 +57,8 @@ def tile_qca_operator_deep_pa_t_kernel(tc, x_cat, w1, out):
         w_sb = const.tile([P, 1024], BF16, name="w_sb")
         nc.gpsimd.dma_start(out=w_sb, in_=w1)
         load_rows(0, 0, ROWS + 1, [nc.sync, nc.scalar])
-        load_rows(0, ROWS + 1, HH, [nc.sync])
+        load_rows(0, ROWS + 1, 2 * ROWS + 1, [nc.sync])
+        load_rows(0, 2 * ROWS + 1, HH, [nc.sync])
         for b in range(1, B):
             load_rows(b, 0, HH, [nc.sync])
 
@@ -115,7 +116,7 @@ def tile_qca_operator_deep_pa_t_kernel(tc, x_cat, w1, out):
             st[i]["vo"] = work.tile([P, NPX], F32, name="vo")
             st[i]["rr"] = work.tile([P, NPX], F32, name="rr")
             if i >= LAG_Q:
-                return add_chain(i, 0, rows, rows - PE_ROWS if offloaded(i) else rows)
+                return add_chain(i, 0, rows, rows - pe_rows(i))
             half = rows // 2
             pairs = zip(add_chain(i, 0, half, half), add_chain(i, half, half, half))
             return [op for pair in pairs for op in pair]
@@ -143,35 +144,38 @@ def tile_qca_operator_deep_pa_t_kernel(tc, x_cat, w1, out):
                 lambda: nc.vector.tensor_tensor(out=rr, in0=rr, in1=vov, op=ADD),
             ]
 
-        def offloaded(i):
-            return i in (2, 4, 6, 8, 10, 12, 13, 14)
+        def pe_rows(i):
+            return PE_ROWS.get(i, 0)
 
         def pe_adds(i):
             rows = chunks[i][2]
-            rv = rows - PE_ROWS
+            rp = pe_rows(i)
+            rv = rows - rp
             vc = vcs[i % 3]
             accn = psn.tile([P, NT], F32, name="accn")
             st[i]["accn"] = accn
             terms = [
-                padded(vc, 3 + rv * PITCH, PE_ROWS),
-                padded(vc, 5 + rv * PITCH, PE_ROWS),
+                padded(vc, 3 + rv * PITCH, rp),
+                padded(vc, 5 + rv * PITCH, rp),
                 rowsof(st[i]["vo"][:, rv * WW : rows * WW]),
             ]
             for k, term in enumerate(terms):
-                nc.tensor.matmul(out=rowsof(accn), lhsT=identf, rhs=term, start=(k == 0), stop=(k == 2))
+                nc.tensor.matmul(
+                    out=rowsof(accn[:, : rp * WW]), lhsT=identf, rhs=term, start=(k == 0), stop=(k == 2)
+                )
 
         def repeat(i):
             n = chunks[i][2] * WW
             rep = work.tile([P, 4 * NPX], BF16, name="rep", align_bytes=64)
-            nv = n - NT if offloaded(i) else n
+            nv = n - pe_rows(i) * WW
             nc.scalar.copy(
                 out=rep[:, : 4 * nv].rearrange("p (n t) -> p n t", t=4),
                 in_=st[i]["rr"][:, :nv].unsqueeze(2).to_broadcast([P, nv, 4]),
             )
-            if offloaded(i):
+            if nv < n:
                 nc.scalar.copy(
                     out=rep[:, 4 * nv : 4 * n].rearrange("p (n t) -> p n t", t=4),
-                    in_=st[i]["accn"].unsqueeze(2).to_broadcast([P, NT, 4]),
+                    in_=st[i]["accn"][:, : n - nv].unsqueeze(2).to_broadcast([P, n - nv, 4]),
                 )
             st[i]["rep"] = rep
 
@@ -234,7 +238,7 @@ def tile_qca_operator_deep_pa_t_kernel(tc, x_cat, w1, out):
                     op1=MIN,
                 )
 
-            return [one(c0, w) for c0, w in spans(i)]
+            return [one(0, chunks[i][2] * WW)]
 
         def store(i):
             b, y0, rows = chunks[i]
@@ -259,7 +263,7 @@ def tile_qca_operator_deep_pa_t_kernel(tc, x_cat, w1, out):
                 if q_ops and k == len(q_ops) - 1:
                     multiply(i - LAG_Q)
                     exps(i - LAG_Q)
-                if a_ops and k == 1 and offloaded(i):
+                if a_ops and k == 1 and pe_rows(i):
                     pe_adds(i)
             if a_ops:
                 repeat(i)

@@ -44,21 +44,18 @@ def tile_qca_operator_deep_pa_t_kernel(tc, x_cat, w1, out):
             nc.vector.memset(xz[b][:, (HH + 1) * WW : (HH + 2) * WW], 0.0)
 
         def load_rows(b, r0, r1, queues):
-            xv = x_cat[b].rearrange("(h a j i) y x -> h a i j (y x)", h=2, a=2, j=8, i=4)
-            for h in range(2):
-                for a in range(2):
-                    for i in range(4):
-                        p0 = 64 * h + 4 * a + i
-                        queues[i % len(queues)].dma_start(
-                            out=xz[b][p0 : 64 * h + 64 : 8, (r0 + 1) * WW : (r1 + 1) * WW],
-                            in_=xv[h, a, i][:, r0 * WW : r1 * WW],
-                        )
+            xv = x_cat[b].rearrange("(h a j i) y x -> a i j h (y x)", h=2, a=2, j=8, i=4)
+            for a in range(2):
+                for i in range(4):
+                    queues[i % len(queues)].dma_start(
+                        out=xz[b][4 * a + i : P : 8, (r0 + 1) * WW : (r1 + 1) * WW],
+                        in_=xv[a, i][:, :, r0 * WW : r1 * WW],
+                    )
 
         w_sb = const.tile([P, 1024], BF16, name="w_sb")
         nc.gpsimd.dma_start(out=w_sb, in_=w1)
         load_rows(0, 0, ROWS + 1, [nc.sync, nc.scalar])
-        load_rows(0, ROWS + 1, 2 * ROWS + 1, [nc.sync])
-        load_rows(0, 2 * ROWS + 1, HH, [nc.sync])
+        load_rows(0, ROWS + 1, HH, [nc.sync])
         for b in range(1, B):
             load_rows(b, 0, HH, [nc.sync])
 
@@ -74,9 +71,7 @@ def tile_qca_operator_deep_pa_t_kernel(tc, x_cat, w1, out):
         for h in range(2):
             for a in range(2):
                 nc.scalar.copy(
-                    out=w_q[:, :, 64 * h : 64 * h + 64].rearrange(
-                        "o r (j a i) -> o r j a i", j=8, a=2, i=4
-                    )[:, :, :, a, :],
+                    out=w_q.rearrange("o r (j h a i) -> o r j h a i", j=8, h=2, a=2, i=4)[:, :, :, h, a, :],
                     in_=w_sb[:, (2 * h + a) * 256 : (2 * h + a + 1) * 256].rearrange(
                         "o (j i r) -> o r j i", j=8, i=4, r=8
                     ),

@@ -23,7 +23,7 @@ NPX = ROWS * WW
 NT = 512
 PE_ROWS = {2: 8, 3: 4, 4: 8, 6: 8, 8: 8, 10: 8, 12: 8, 13: 8, 14: 8}
 LAG_Q = 2
-LAG_F = 3
+LAG_F = 4
 
 FLOPS = 2 * B * PIX * 1024 * P
 
@@ -32,7 +32,7 @@ def tile_qca_operator_deep_pa_t_kernel(tc, x_cat, w1, out):
     nc = tc.nc
     with ExitStack() as ctx:
         const = ctx.enter_context(tc.tile_pool(name="const", bufs=1))
-        work = ctx.enter_context(tc.tile_pool(name="work", bufs=3))
+        work = ctx.enter_context(tc.tile_pool(name="work", bufs=4))
         psw = ctx.enter_context(tc.psum_pool(name="psw", bufs=1))
         psum = ctx.enter_context(tc.psum_pool(name="psum", bufs=5))
         psn = ctx.enter_context(tc.psum_pool(name="psn", bufs=2))
@@ -55,7 +55,8 @@ def tile_qca_operator_deep_pa_t_kernel(tc, x_cat, w1, out):
         w_sb = const.tile([P, 1024], BF16, name="w_sb")
         nc.gpsimd.dma_start(out=w_sb, in_=w1)
         load_rows(0, 0, ROWS + 1, [nc.sync, nc.scalar])
-        load_rows(0, ROWS + 1, HH, [nc.sync])
+        load_rows(0, ROWS + 1, 2 * ROWS + 1, [nc.sync])
+        load_rows(0, 2 * ROWS + 1, HH, [nc.sync])
         for b in range(1, B):
             load_rows(b, 0, HH, [nc.sync])
 
@@ -63,9 +64,9 @@ def tile_qca_operator_deep_pa_t_kernel(tc, x_cat, w1, out):
         make_identity(nc, ident)
         identf = const.tile([P, P], F32, name="identf")
         make_identity(nc, identf)
-        vcs = [const.tile([P, ROWS * PITCH + 8], F32, name="vc%d" % k) for k in range(3)]
+        vcs = [const.tile([P, (ROWS + 1) * PITCH], F32, name="vc%d" % k) for k in range(3)]
         for k in range(3):
-            nc.gpsimd.memset(vcs[k], 0.0)
+            nc.vector.memset(vcs[k].rearrange("p (r c) -> p r c", c=PITCH)[:, :, 0:4], 0.0)
 
         w_q = const.tile([P, 8, P], BF16, name="w_q")
         for h in range(2):

@@ -21,7 +21,7 @@ PITCH = 68
 ROWS = 16
 NPX = ROWS * WW
 NT = 512
-PE_ROWS = {2: 8, 3: 4, 4: 8, 6: 8, 8: 8, 10: 8, 12: 8, 13: 8, 14: 8}
+PE_ROWS = {3: 4, 4: 8, 5: 8, 6: 8, 8: 8, 10: 8, 12: 8, 13: 8, 14: 8}
 LAG_Q = 2
 LAG_F = 4
 
@@ -81,7 +81,10 @@ def tile_qca_operator_deep_pa_t_kernel(tc, x_cat, w1, out):
         for r in range(8):
             nc.tensor.transpose(w_t[:, r, :], w_q[:, r, :], ident)
         w_g = const.tile([P, 2, P, 4], BF16, name="w_g", align_bytes=64)
-        nc.scalar.copy(out=w_g, in_=w_t.rearrange("p (g t) o -> p g o t", g=2, t=4))
+
+        def regroup_w():
+            nc.scalar.copy(out=w_g, in_=w_t.rearrange("p (g t) o -> p g o t", g=2, t=4))
+
         w_codes = const.tile([P, 2 * P], U32, name="w_codes", align_bytes=64)
         w_scl = const.tile([P, 2 * P], U8, name="w_scl", align_bytes=64)
 
@@ -248,20 +251,23 @@ def tile_qca_operator_deep_pa_t_kernel(tc, x_cat, w1, out):
             a_ops = add_ops(i) if i < nch else []
             q_ops = quant_ops(i - LAG_Q) if 0 <= i - LAG_Q < nch else []
             f_ops = finish_ops(i - LAG_F) if 0 <= i - LAG_F < nch else []
-            if i == LAG_Q:
-                quantise_w()
             others = q_ops + f_ops
+            if i == LAG_Q:
+                others = [q_ops[0], quantise_w, q_ops[1]]
+            ready = len(others) - len(f_ops) - 1
             for k in range(max(len(a_ops), len(others))):
                 if k < len(a_ops):
                     a_ops[k]()
                 if k < len(others):
                     others[k]()
-                if q_ops and k == len(q_ops) - 1:
+                if q_ops and k == ready:
                     multiply(i - LAG_Q)
                     exps(i - LAG_Q)
                 if a_ops and k == 1 and pe_rows(i):
                     pe_adds(i)
             if a_ops:
                 repeat(i)
+            if i == 0:
+                regroup_w()
             if f_ops:
                 store(i - LAG_F)

@@ -10,6 +10,7 @@ U32 = mybir.dt.uint32
 U8 = mybir.dt.uint8
 ADD = mybir.AluOpType.add
 MIN = mybir.AluOpType.min
+MAX = mybir.AluOpType.max
 ACT = mybir.ActivationFunctionType
 
 P = 128
@@ -17,13 +18,21 @@ B = 4
 HH = 64
 WW = 64
 PIX = HH * WW
-PITCH = 68
-ROWS = 16
-NPX = ROWS * WW
+NPX = 1024
 NT = 512
-PE_ROWS = {3: 4, 4: 8, 5: 8, 6: 8, 8: 8, 10: 8, 12: 8, 13: 8, 14: 8}
-LAG_Q = 2
-LAG_F = 4
+
+PR, PC = 7, 18
+STEP = PR - 2
+COL0 = (0, 15, 31, 46)
+SC = 16
+RT = 10
+PE_ROWS = 1 + RT * STEP
+XN_ROWS = (RT - 1) * STEP + PR + 2
+HEAD_ROWS = 24
+
+V0 = PE_ROWS
+VR = HH - PE_ROWS
+PITCH = 68
 
 FLOPS = 2 * B * PIX * 1024 * P
 
@@ -33,150 +42,225 @@ def tile_qca_operator_deep_pa_t_kernel(tc, x_cat, w1, out):
     with ExitStack() as ctx:
         const = ctx.enter_context(tc.tile_pool(name="const", bufs=1))
         work = ctx.enter_context(tc.tile_pool(name="work", bufs=4))
-        psw = ctx.enter_context(tc.psum_pool(name="psw", bufs=1))
-        psum = ctx.enter_context(tc.psum_pool(name="psum", bufs=5))
+        xpool = ctx.enter_context(tc.tile_pool(name="xpool", bufs=6))
+        psum = ctx.enter_context(tc.psum_pool(name="psum", bufs=4))
         psn = ctx.enter_context(tc.psum_pool(name="psn", bufs=2))
+        pst = ctx.enter_context(tc.psum_pool(name="pst", bufs=2))
         ctx.enter_context(tc.manual_schedule())
 
-        xz = [const.tile([P, (HH + 2) * WW], BF16, name="xz%d" % b) for b in range(B)]
-        for b in range(B):
-            nc.vector.memset(xz[b][:, 0:WW], 0.0)
-            nc.vector.memset(xz[b][:, (HH + 1) * WW : (HH + 2) * WW], 0.0)
+        x_nat = [const.tile([P, XN_ROWS * WW], BF16, name="xn%d" % b) for b in range(B)]
+        x_bot = [const.tile([P, (VR + 2) * WW], BF16, name="xb%d" % b) for b in range(B)]
 
-        def load_rows(b, r0, r1, queues):
-            xv = x_cat[b].rearrange("(h a j i) y x -> a i j h (y x)", h=2, a=2, j=8, i=4)
-            for a in range(2):
-                for i in range(4):
-                    queues[i % len(queues)].dma_start(
-                        out=xz[b][4 * a + i : P : 8, (r0 + 1) * WW : (r1 + 1) * WW],
-                        in_=xv[a, i][:, :, r0 * WW : r1 * WW],
-                    )
+        def load_nat(b, r0, r1):
+            nc.sync.dma_start(
+                out=x_nat[b][:, r0 * WW : r1 * WW],
+                in_=x_cat[b].rearrange("c y x -> c (y x)")[:, r0 * WW : r1 * WW],
+            )
+
+        def load_bot(b):
+            xv = x_cat[b].rearrange("(q w m) y x -> w q m (y x)", q=4, w=2, m=16)
+            for w in range(2):
+                nc.sync.dma_start(out=x_bot[b][w:P:2, 0 : (VR + 1) * WW], in_=xv[w][:, :, (V0 - 1) * WW : PIX])
 
         w_sb = const.tile([P, 1024], BF16, name="w_sb")
-        nc.gpsimd.dma_start(out=w_sb, in_=w1)
-        load_rows(0, 0, ROWS + 1, [nc.sync, nc.scalar])
-        load_rows(0, ROWS + 1, 2 * ROWS + 1, [nc.sync])
-        load_rows(0, 2 * ROWS + 1, HH, [nc.sync])
+        load_nat(0, 0, HEAD_ROWS)
+        nc.scalar.dma_start(out=w_sb, in_=w1)
+        load_bot(0)
+        load_nat(0, HEAD_ROWS, XN_ROWS)
+        load_bot(1)
         for b in range(1, B):
-            load_rows(b, 0, HH, [nc.sync])
+            load_nat(b, 0, XN_ROWS)
+            if b > 1:
+                load_bot(b)
 
         ident = const.tile([P, P], BF16, name="ident")
         make_identity(nc, ident)
-        identf = const.tile([P, P], F32, name="identf")
-        make_identity(nc, identf)
-        vcs = [const.tile([P, (ROWS + 1) * PITCH], F32, name="vc%d" % k) for k in range(3)]
-        for k in range(3):
+        for b in range(B):
+            nc.vector.memset(x_bot[b][:, (VR + 1) * WW :], 0.0)
+        vcs = [const.tile([P, (VR + 1) * PITCH], F32, name="vc%d" % k) for k in range(2)]
+        for k in range(2):
             nc.vector.memset(vcs[k].rearrange("p (r c) -> p r c", c=PITCH)[:, :, 0:4], 0.0)
+        idp = const.tile([P, PR + 2, PC + 2], BF16, name="idp")
+        nc.vector.memset(idp, 0.0)
+        perm = const.tile([P, P], BF16, name="perm")
+        nc.vector.tensor_copy(
+            out=perm.rearrange("k (q m w) -> k q m w", q=4, m=16, w=2),
+            in_=ident.rearrange("k (q w m) -> k q m w", q=4, w=2, m=16),
+        )
+        nc.vector.tensor_copy(
+            out=idp[:, 1 : PR + 1, 1 : PC + 1], in_=ident[:, : PR * PC].rearrange("p (r c) -> p r c", c=PC)
+        )
+        nv1 = const.tile([P, PR, PC + 2], BF16, name="nv1")
+        nv2 = const.tile([P, PR, PC + 2], BF16, name="nv2")
+        nh = const.tile([P, PR, PC], BF16, name="nh")
+        nmat = const.tile([P, PR, PC], BF16, name="nmat")
+        nc.vector.tensor_tensor(out=nv1, in0=idp[:, 0:PR, :], in1=idp[:, 2 : PR + 2, :], op=ADD)
+        nc.vector.tensor_tensor(out=nv2, in0=nv1, in1=idp[:, 1 : PR + 1, :], op=ADD)
+        nc.vector.tensor_tensor(out=nh, in0=nv2[:, :, 0:PC], in1=nv2[:, :, 2 : PC + 2], op=ADD)
+        nc.vector.tensor_tensor(out=nmat, in0=nh, in1=nv1[:, :, 1 : PC + 1], op=ADD)
 
         w_q = const.tile([P, 8, P], BF16, name="w_q")
-        for h in range(2):
-            for a in range(2):
-                nc.scalar.copy(
-                    out=w_q.rearrange("o r (j h a i) -> o r j h a i", j=8, h=2, a=2, i=4)[:, :, :, h, a, :],
-                    in_=w_sb[:, (2 * h + a) * 256 : (2 * h + a + 1) * 256].rearrange(
-                        "o (j i r) -> o r j i", j=8, i=4, r=8
-                    ),
-                )
-        w_t = psw.tile([P, 8, P], BF16, name="w_t")
-        for r in range(8):
-            nc.tensor.transpose(w_t[:, r, :], w_q[:, r, :], ident)
         w_g = const.tile([P, 2, P, 4], BF16, name="w_g", align_bytes=64)
-
-        def regroup_w():
-            nc.scalar.copy(out=w_g, in_=w_t.rearrange("p (g t) o -> p g o t", g=2, t=4))
-
         w_codes = const.tile([P, 2 * P], U32, name="w_codes", align_bytes=64)
         w_scl = const.tile([P, 2 * P], U8, name="w_scl", align_bytes=64)
 
+        def prepare_w():
+            for q in range(4):
+                nc.scalar.copy(
+                    out=w_q[:, :, 32 * q : 32 * q + 32].rearrange("o r (m w) -> o r m w", m=16, w=2),
+                    in_=w_sb[:, 256 * q : 256 * q + 256].rearrange("o (w m r) -> o r m w", w=2, m=16, r=8),
+                )
+            w_t = pst.tile([P, 8, P], BF16, name="xt_ps")
+            for r in range(8):
+                nc.tensor.transpose(w_t[:, r, :], w_q[:, r, :], ident)
+            nc.scalar.copy(out=w_g, in_=w_t.rearrange("p (g t) o -> p g o t", g=2, t=4))
+
         def quantise_w():
             nc.vector.quantize_mx(
-                out=w_codes.bitcast(FP8X4),
-                scales=w_scl,
-                in_=w_g.rearrange("p g o t -> p (g o t)"),
+                out=w_codes.bitcast(FP8X4), scales=w_scl, in_=w_g.rearrange("p g o t -> p (g o t)")
             )
 
-        def padded(t, off, rows):
-            return t[:, off : off + rows * PITCH].rearrange("p (r c) -> p r c", c=PITCH)[:, :, 0:WW]
+        strips = {}
+        xts = {}
 
-        def rowsof(ap):
-            return ap.rearrange("p (r c) -> p r c", c=WW)
+        def strip_ops(b, r0, r1):
+            if b not in strips:
+                strips[b] = work.tile([P, 4, XN_ROWS * PC], BF16, name="strips")
+
+            def one(s):
+                src = x_nat[b].rearrange("p (y x) -> p y x", x=WW)
+                views = []
+                for k in (s, s + 1):
+                    views.append(src[:, r0:r1, COL0[k] : COL0[k] + PC])
+
+                def go(k):
+                    return lambda: nc.vector.tensor_copy(
+                        out=strips[b][:, s + k, r0 * PC : r1 * PC].rearrange("p (y x) -> p y x", x=PC), in_=views[k]
+                    )
+
+                return [go(0), go(1)]
+
+            return one(0) + one(2)
+
+        def transpose_pair(b, pair):
+            ps = pst.tile([P, 8, P], BF16, name="xt_ps")
+            for k in range(2):
+                r0 = (2 * pair + k) * STEP
+                for s in range(4):
+                    nc.tensor.transpose(ps[:, 4 * k + s, :], strips[b][:, s, r0 * PC : r0 * PC + P], perm)
+            return ps
+
+        def copy_pair(b, pair, ps):
+            xt = xpool.tile([P, 8, P], BF16, name="xt")
+            nc.scalar.copy(out=xt, in_=ps)
+            xts[b, pair] = xt
 
         chunks = []
         for b in range(B):
-            sizes = [16, 16, 16, 16] if b < B - 1 else [16, 16, 16, 8, 4, 4]
+            sizes = [16, 16, 16, 16]
+            if b == 0:
+                sizes = [4, 4, 8, 16, 16, 16]
+            if b == B - 1:
+                sizes = [16, 16, 16, 8, 4, 4]
             y0 = 0
             for rows in sizes:
                 chunks.append((b, y0, rows))
                 y0 += rows
+        nch = len(chunks)
         st = [dict() for c in chunks]
+        first = [min(i for i in range(nch) if chunks[i][0] == b) for b in range(B)]
+        bottom = [min(i for i in range(nch) if chunks[i][0] == b and chunks[i][1] + chunks[i][2] > V0) for b in range(B)]
 
-        def add_ops(i):
-            rows = chunks[i][2]
-            st[i]["vo"] = work.tile([P, NPX], F32, name="vo")
-            st[i]["rr"] = work.tile([P, NPX], F32, name="rr")
-            if i >= LAG_Q:
-                return add_chain(i, 0, rows, rows - pe_rows(i))
-            half = rows // 2
-            pairs = zip(add_chain(i, 0, half, half), add_chain(i, half, half, half))
-            return [op for pair in pairs for op in pair]
+        def pe_count(i):
+            b, y0, rows = chunks[i]
+            return max(0, min(y0 + rows, PE_ROWS) - y0) * WW
 
-        def add_chain(i, ra, rows, rv):
-            b, y0, all_rows = chunks[i]
-            ya = y0 + ra
-            n = rows * WW
-            vc = vcs[i % 3]
-            up = xz[b][:, ya * WW : ya * WW + n]
-            mid = xz[b][:, (ya + 1) * WW : (ya + 1) * WW + n]
-            dn = xz[b][:, (ya + 2) * WW : (ya + 2) * WW + n]
-            vo = st[i]["vo"][:, ra * WW : ra * WW + n]
-            vov = st[i]["vo"][:, ra * WW : (ra + rv) * WW]
-            rr = st[i]["rr"][:, ra * WW : (ra + rv) * WW]
-            off = ra * PITCH
+        def pairs_of(i):
+            b, y0, rows = chunks[i]
+            y1 = min(y0 + rows, PE_ROWS)
+            if y1 <= y0:
+                return []
+            lo = max(0, (y0 - 1) // STEP)
+            hi = max(0, (y1 - 2) // STEP)
+            return list(range(lo // 2, hi // 2 + 1))
+
+        def patch_sums(i):
+            b, y0, rows = chunks[i]
+            n = pe_count(i)
+            if n == 0:
+                return
+            nb = psn.tile([P, NPX], BF16, name="nb")
+            st[i]["nb"] = nb
+            nb3 = nb.rearrange("p (y x) -> p y x", x=WW)
+            for rt in range(RT):
+                r0 = rt * STEP
+                ya = max(y0, r0 + 1 if rt else 0)
+                yb = min(y0 + rows, r0 + PR - 1)
+                if yb <= ya:
+                    continue
+                for s in range(4):
+                    c0 = SC * s - COL0[s]
+                    nc.tensor.matmul(
+                        out=nb3[:, ya - y0 : yb - y0, SC * s : SC * s + SC],
+                        lhsT=xts[b, rt // 2][:, 4 * (rt % 2) + s, :],
+                        rhs=nmat[:, ya - r0 : yb - r0, c0 : c0 + SC],
+                        start=True,
+                        stop=True,
+                    )
+
+        nbv = [const.tile([P, VR * WW], BF16, name="nbv%d" % b) for b in range(B)]
+
+        def rowsof(ap):
+            return ap.rearrange("p (r c) -> p r c", c=WW)
+
+        def add_ops(b):
+            n = VR * WW
+            vc = vcs[b % 2].rearrange("p (r c) -> p r c", c=PITCH)
+            flat = vcs[b % 2]
+            vo = work.tile([P, VR * WW], F32, name="vo")
+            rr = work.tile([P, VR * WW], F32, name="rr")
+
+            def shifted(off):
+                return flat[:, off : off + VR * PITCH].rearrange("p (r c) -> p r c", c=PITCH)[:, :, 0:WW]
+
             return [
-                lambda: nc.vector.tensor_tensor(out=vo, in0=up, in1=dn, op=ADD),
                 lambda: nc.vector.tensor_tensor(
-                    out=padded(vc, off + 4, rows), in0=rowsof(vo), in1=rowsof(mid), op=ADD
+                    out=vo, in0=x_bot[b][:, 0:n], in1=x_bot[b][:, 2 * WW : 2 * WW + n], op=ADD
                 ),
                 lambda: nc.vector.tensor_tensor(
-                    out=rowsof(rr), in0=padded(vc, off + 3, rv), in1=padded(vc, off + 5, rv), op=ADD
+                    out=shifted(4), in0=rowsof(vo), in1=rowsof(x_bot[b][:, WW : WW + n]), op=ADD
                 ),
-                lambda: nc.vector.tensor_tensor(out=rr, in0=rr, in1=vov, op=ADD),
+                lambda: nc.vector.tensor_tensor(out=rowsof(rr), in0=shifted(3), in1=shifted(5), op=ADD),
+                lambda: nc.vector.tensor_tensor(out=nbv[b], in0=rr, in1=vo, op=ADD),
             ]
 
-        def pe_rows(i):
-            return PE_ROWS.get(i, 0)
+        def rep_tile(i):
+            if "rep" not in st[i]:
+                st[i]["rep"] = work.tile([P, 4 * NPX], BF16, name="rep", align_bytes=64)
+            return st[i]["rep"]
 
-        def pe_adds(i):
-            rows = chunks[i][2]
-            rp = pe_rows(i)
-            rv = rows - rp
-            vc = vcs[i % 3]
-            accn = psn.tile([P, NT], F32, name="accn")
-            st[i]["accn"] = accn
-            terms = [
-                padded(vc, 3 + rv * PITCH, rp),
-                padded(vc, 5 + rv * PITCH, rp),
-                rowsof(st[i]["vo"][:, rv * WW : rows * WW]),
-            ]
-            for k, term in enumerate(terms):
-                nc.tensor.matmul(
-                    out=rowsof(accn[:, : rp * WW]), lhsT=identf, rhs=term, start=(k == 0), stop=(k == 2)
-                )
-
-        def repeat(i):
-            n = chunks[i][2] * WW
-            rep = work.tile([P, 4 * NPX], BF16, name="rep", align_bytes=64)
-            nv = n - pe_rows(i) * WW
-            nc.scalar.copy(
-                out=rep[:, : 4 * nv].rearrange("p (n t) -> p n t", t=4),
-                in_=st[i]["rr"][:, :nv].unsqueeze(2).to_broadcast([P, nv, 4]),
-            )
-            if nv < n:
+        def repeat_scalar(i):
+            n = pe_count(i)
+            if n:
                 nc.scalar.copy(
-                    out=rep[:, 4 * nv : 4 * n].rearrange("p (n t) -> p n t", t=4),
-                    in_=st[i]["accn"][:, : n - nv].unsqueeze(2).to_broadcast([P, n - nv, 4]),
+                    out=rep_tile(i)[:, : 4 * n].rearrange("p (n t) -> p n t", t=4),
+                    in_=st[i]["nb"][:, :n].unsqueeze(2).to_broadcast([P, n, 4]),
                 )
-            st[i]["rep"] = rep
+
+        def repeat_vector(i):
+            b, y0, rows = chunks[i]
+            n0 = pe_count(i)
+            n = rows * WW - n0
+            if n == 0:
+                return []
+            a = (y0 - V0) * WW + n0
+            rep = rep_tile(i)
+            return [
+                lambda: nc.vector.tensor_copy(
+                    out=rep[:, 4 * n0 : 4 * (n0 + n)].rearrange("p (n t) -> p n t", t=4),
+                    in_=nbv[b][:, a : a + n].unsqueeze(2).to_broadcast([P, n, 4]),
+                )
+            ]
 
         def quant_ops(i):
             n = chunks[i][2] * WW
@@ -184,10 +268,11 @@ def tile_qca_operator_deep_pa_t_kernel(tc, x_cat, w1, out):
             scl = work.tile([P, 2, NPX], U8, name="scl", align_bytes=64)
             st[i]["codes"] = codes
             st[i]["scl"] = scl
+            rep = st[i]["rep"]
 
             def one(g):
                 return lambda: nc.vector.quantize_mx(
-                    out=codes[:, g, :n].bitcast(FP8X4), scales=scl[:, g, :n], in_=st[i]["rep"][:, : 4 * n]
+                    out=codes[:, g, :n].bitcast(FP8X4), scales=scl[:, g, :n], in_=rep[:, : 4 * n]
                 )
 
             return [one(0), one(1)]
@@ -217,57 +302,84 @@ def tile_qca_operator_deep_pa_t_kernel(tc, x_cat, w1, out):
 
         def exps(i):
             ee = work.tile([P, NPX], F32, name="ee")
-            oo = work.tile([P, NPX], F32, name="oo")
             for k, (c0, w) in enumerate(spans(i)):
                 nc.scalar.activation(out=ee[:, c0 : c0 + w], in_=st[i]["accs"][k][:, :w], func=ACT.Exp)
-                nc.scalar.activation(out=oo[:, c0 : c0 + w], in_=st[i]["accs"][k][:, :w], func=ACT.Relu)
             st[i]["ee"] = ee
-            st[i]["oo"] = oo
 
-        def finish_ops(i):
-            oo = st[i]["oo"]
+        def clamp_ops(i):
+            n = chunks[i][2] * WW
+            ee = st[i]["ee"]
+            return [
+                lambda: nc.vector.tensor_scalar(
+                    out=ee[:, :n], in0=ee[:, :n], scalar1=1.0, scalar2=-1.0, op0=MIN, op1=ADD
+                )
+            ]
 
-            def one(c0, w):
-                return lambda: nc.vector.scalar_tensor_tensor(
-                    out=oo[:, c0 : c0 + w],
-                    in0=st[i]["ee"][:, c0 : c0 + w],
-                    scalar=-1.0,
-                    in1=oo[:, c0 : c0 + w],
-                    op0=ADD,
-                    op1=MIN,
+        def max_ops(i):
+            ee = st[i]["ee"]
+
+            def one(k, c0, w):
+                return lambda: nc.vector.tensor_tensor(
+                    out=ee[:, c0 : c0 + w], in0=ee[:, c0 : c0 + w], in1=st[i]["accs"][k][:, :w], op=MAX
                 )
 
-            return [one(0, chunks[i][2] * WW)]
+            return [one(k, c0, w) for k, (c0, w) in enumerate(spans(i))]
 
         def store(i):
             b, y0, rows = chunks[i]
             n = rows * WW
             nc.sync.dma_start(
-                out=out[b].rearrange("o y x -> o (y x)")[:, y0 * WW : y0 * WW + n], in_=st[i]["oo"][:, :n]
+                out=out[b].rearrange("o y x -> o (y x)")[:, y0 * WW : y0 * WW + n], in_=st[i]["ee"][:, :n]
             )
 
-        nch = len(chunks)
-        for i in range(nch + LAG_F):
-            a_ops = add_ops(i) if i < nch else []
-            q_ops = quant_ops(i - LAG_Q) if 0 <= i - LAG_Q < nch else []
-            f_ops = finish_ops(i - LAG_F) if 0 <= i - LAG_F < nch else []
-            others = q_ops + f_ops
-            if i == LAG_Q:
-                others = [q_ops[0], quantise_w, q_ops[1]]
-            ready = len(others) - len(f_ops) - 1
-            for k in range(max(len(a_ops), len(others))):
-                if k < len(a_ops):
-                    a_ops[k]()
-                if k < len(others):
-                    others[k]()
-                if q_ops and k == ready:
-                    multiply(i - LAG_Q)
-                    exps(i - LAG_Q)
-                if a_ops and k == 1 and pe_rows(i):
-                    pe_adds(i)
-            if a_ops:
-                repeat(i)
-            if i == 0:
-                regroup_w()
-            if f_ops:
-                store(i - LAG_F)
+        extra = {}
+
+        def put(i, ops):
+            extra.setdefault(i, []).extend(ops)
+
+        for op in strip_ops(0, 0, HEAD_ROWS):
+            op()
+        adds = [add_ops(b) for b in range(B)]
+        put(-3, strip_ops(0, HEAD_ROWS, XN_ROWS))
+        put(-2, adds[0][:2])
+        put(-1, adds[0][2:])
+        put(-1, [quantise_w])
+        for k in range(4):
+            put(k, [adds[1][k]])
+        for b in range(1, B):
+            for k, op in enumerate(strip_ops(b, 0, XN_ROWS)):
+                put(first[b] - 5 + k // 2, [op])
+            if b > 1:
+                for k in range(4):
+                    put(bottom[b] - 4 + k, [adds[b][k]])
+
+        def at(i, f):
+            return f(i) if 0 <= i < nch else []
+
+        done = set()
+
+        def transposes(i):
+            new = []
+            b = chunks[i][0]
+            for pair in pairs_of(i):
+                if (b, pair) not in done:
+                    done.add((b, pair))
+                    new.append((b, pair, transpose_pair(b, pair)))
+            return new
+
+        for i in range(-3, nch + 3):
+            at(i + 1, patch_sums)
+            at(i - 2, multiply)
+            new = at(i + 3, transposes)
+            if i == -2:
+                prepare_w()
+            at(i + 1, repeat_scalar)
+            at(i - 2, exps)
+            for b, pair, ps in new:
+                copy_pair(b, pair, ps)
+            q = at(i - 1, quant_ops)
+            m = at(i - 3, max_ops)
+            queue = at(i - 3, clamp_ops) + at(i, repeat_vector) + q[:1] + m[:1] + q[1:] + m[1:] + extra.get(i, [])
+            for op in queue:
+                op()
+            at(i - 3, store)

@@ -106,7 +106,7 @@ def tile_qca_operator_deep_pa_t_kernel(tc, x_cat, w1, out):
 
         def prepare_w():
             for q in range(4):
-                nc.scalar.copy(
+                nc.vector.tensor_copy(
                     out=w_q[:, :, 32 * q : 32 * q + 32].rearrange("o r (m w) -> o r m w", m=16, w=2),
                     in_=w_sb[:, 256 * q : 256 * q + 256].rearrange("o (w m r) -> o r m w", w=2, m=16, r=8),
                 )
@@ -155,29 +155,34 @@ def tile_qca_operator_deep_pa_t_kernel(tc, x_cat, w1, out):
             nc.scalar.copy(out=xt, in_=ps)
             xts[b, pair] = xt
 
+        plan = [
+            [(0, 0, 8), (8, 0, 0), (14, 0, 2), (14, 0, 2), (15, 0, 1)],
+            [(13, 0, 3), (13, 0, 3), (13, 0, 3), (12, 0, 4)],
+            [(13, 0, 3), (13, 0, 3), (13, 0, 3), (12, 0, 4)],
+            [(13, 0, 3), (13, 0, 3), (13, 0, 3), (4, 0, 4), (4, 0, 0), (4, 0, 0)],
+        ]
         chunks = []
+        share = []
         for b in range(B):
-            sizes = [16, 16, 16, 16]
-            if b == 0:
-                sizes = [4, 4, 8, 16, 16, 16]
-            if b == B - 1:
-                sizes = [16, 16, 16, 8, 4, 4]
-            y0 = 0
-            for rows in sizes:
-                chunks.append((b, y0, rows))
-                y0 += rows
+            pa, va = 0, V0
+            for np_, nr, nv in plan[b]:
+                chunks.append((b, pa, pa + np_, va, va + nv))
+                share.append(nr * WW)
+                pa += np_
+                va += nv
         nch = len(chunks)
         st = [dict() for c in chunks]
         first = [min(i for i in range(nch) if chunks[i][0] == b) for b in range(B)]
-        bottom = [min(i for i in range(nch) if chunks[i][0] == b and chunks[i][1] + chunks[i][2] > V0) for b in range(B)]
+        bottom = [min(i for i in range(nch) if chunks[i][0] == b and chunks[i][4] > chunks[i][3]) for b in range(B)]
 
         def pe_count(i):
-            b, y0, rows = chunks[i]
-            return max(0, min(y0 + rows, PE_ROWS) - y0) * WW
+            return (chunks[i][2] - chunks[i][1]) * WW
+
+        def px_count(i):
+            return pe_count(i) + (chunks[i][4] - chunks[i][3]) * WW
 
         def pairs_of(i):
-            b, y0, rows = chunks[i]
-            y1 = min(y0 + rows, PE_ROWS)
+            b, y0, y1, va, vb = chunks[i]
             if y1 <= y0:
                 return []
             lo = max(0, (y0 - 1) // STEP)
@@ -185,7 +190,7 @@ def tile_qca_operator_deep_pa_t_kernel(tc, x_cat, w1, out):
             return list(range(lo // 2, hi // 2 + 1))
 
         def patch_sums(i):
-            b, y0, rows = chunks[i]
+            b, y0, y1, va, vb = chunks[i]
             n = pe_count(i)
             if n == 0:
                 return
@@ -195,7 +200,7 @@ def tile_qca_operator_deep_pa_t_kernel(tc, x_cat, w1, out):
             for rt in range(RT):
                 r0 = rt * STEP
                 ya = max(y0, r0 + 1 if rt else 0)
-                yb = min(y0 + rows, r0 + PR - 1)
+                yb = min(y1, r0 + PR - 1)
                 if yb <= ya:
                     continue
                 for s in range(4):
@@ -240,7 +245,11 @@ def tile_qca_operator_deep_pa_t_kernel(tc, x_cat, w1, out):
             return st[i]["rep"]
 
         def repeat_scalar(i):
-            n = pe_count(i)
+            n = pe_count(i) - share[i]
+            if share[i]:
+                nbs = work.tile([P, NPX], BF16, name="nbs")
+                nc.scalar.copy(out=nbs[:, : share[i]], in_=st[i]["nb"][:, n : n + share[i]])
+                st[i]["nbs"] = nbs
             if n:
                 nc.scalar.copy(
                     out=rep_tile(i)[:, : 4 * n].rearrange("p (n t) -> p n t", t=4),
@@ -248,22 +257,27 @@ def tile_qca_operator_deep_pa_t_kernel(tc, x_cat, w1, out):
                 )
 
         def repeat_vector(i):
-            b, y0, rows = chunks[i]
+            b, y0, y1, va, vb = chunks[i]
             n0 = pe_count(i)
-            n = rows * WW - n0
-            if n == 0:
-                return []
-            a = (y0 - V0) * WW + n0
+            n = (vb - va) * WW
+            a = (va - V0) * WW
             rep = rep_tile(i)
-            return [
-                lambda: nc.vector.tensor_copy(
-                    out=rep[:, 4 * n0 : 4 * (n0 + n)].rearrange("p (n t) -> p n t", t=4),
-                    in_=nbv[b][:, a : a + n].unsqueeze(2).to_broadcast([P, n, 4]),
+
+            def one(src, at_, n):
+                return lambda: nc.vector.tensor_copy(
+                    out=rep[:, 4 * at_ : 4 * (at_ + n)].rearrange("p (n t) -> p n t", t=4),
+                    in_=src.unsqueeze(2).to_broadcast([P, n, 4]),
                 )
-            ]
+
+            ops = []
+            if share[i]:
+                ops.append(one(st[i]["nbs"][:, : share[i]], n0 - share[i], share[i]))
+            if n:
+                ops.append(one(nbv[b][:, a : a + n], n0, n))
+            return ops
 
         def quant_ops(i):
-            n = chunks[i][2] * WW
+            n = px_count(i)
             codes = work.tile([P, 2, NPX], U32, name="codes", align_bytes=64)
             scl = work.tile([P, 2, NPX], U8, name="scl", align_bytes=64)
             st[i]["codes"] = codes
@@ -278,27 +292,27 @@ def tile_qca_operator_deep_pa_t_kernel(tc, x_cat, w1, out):
             return [one(0), one(1)]
 
         def spans(i):
-            n = chunks[i][2] * WW
+            n = px_count(i)
             return [(c0, min(NT, n - c0)) for c0 in range(0, n, NT)]
 
-        def multiply(i):
+        def multiply(i, g):
             codes = st[i]["codes"]
             scl = st[i]["scl"]
-            accs = []
-            for c0, w in spans(i):
-                acc = psum.tile([P, NT], F32, name="acc")
-                accs.append(acc)
-                for g in range(2):
-                    nc.tensor.matmul_mx(
-                        out=acc[:, :w],
-                        lhsT=w_codes[:, g * P : (g + 1) * P].bitcast(FP8X4),
-                        lhsT_scale=w_scl[:, g * P : (g + 1) * P],
-                        rhs=codes[:, g, c0 : c0 + w].bitcast(FP8X4),
-                        rhs_scale=scl[:, g, c0 : c0 + w],
-                        start=(g == 0),
-                        stop=(g == 1),
-                    )
-            st[i]["accs"] = accs
+            if g == 0:
+                st[i]["accs"] = []
+            for k, (c0, w) in enumerate(spans(i)):
+                if g == 0:
+                    acc = psum.tile([P, NT], F32, name="acc")
+                    st[i]["accs"].append(acc)
+                nc.tensor.matmul_mx(
+                    out=st[i]["accs"][k][:, :w],
+                    lhsT=w_codes[:, g * P : (g + 1) * P].bitcast(FP8X4),
+                    lhsT_scale=w_scl[:, g * P : (g + 1) * P],
+                    rhs=codes[:, g, c0 : c0 + w].bitcast(FP8X4),
+                    rhs_scale=scl[:, g, c0 : c0 + w],
+                    start=(g == 0),
+                    stop=(g == 1),
+                )
 
         def exps(i):
             ee = work.tile([P, NPX], F32, name="ee")
@@ -307,7 +321,7 @@ def tile_qca_operator_deep_pa_t_kernel(tc, x_cat, w1, out):
             st[i]["ee"] = ee
 
         def clamp_ops(i):
-            n = chunks[i][2] * WW
+            n = px_count(i)
             ee = st[i]["ee"]
             return [
                 lambda: nc.vector.tensor_scalar(
@@ -326,11 +340,16 @@ def tile_qca_operator_deep_pa_t_kernel(tc, x_cat, w1, out):
             return [one(k, c0, w) for k, (c0, w) in enumerate(spans(i))]
 
         def store(i):
-            b, y0, rows = chunks[i]
-            n = rows * WW
-            nc.sync.dma_start(
-                out=out[b].rearrange("o y x -> o (y x)")[:, y0 * WW : y0 * WW + n], in_=st[i]["ee"][:, :n]
-            )
+            b, y0, y1, va, vb = chunks[i]
+            at_ = 0
+            for ya, yb in ((y0, y1), (va, vb)):
+                n = (yb - ya) * WW
+                if n:
+                    nc.sync.dma_start(
+                        out=out[b].rearrange("o y x -> o (y x)")[:, ya * WW : yb * WW],
+                        in_=st[i]["ee"][:, at_ : at_ + n],
+                    )
+                at_ += n
 
         extra = {}
 
@@ -356,6 +375,10 @@ def tile_qca_operator_deep_pa_t_kernel(tc, x_cat, w1, out):
         def at(i, f):
             return f(i) if 0 <= i < nch else []
 
+        def run(ops):
+            for op in ops:
+                op()
+
         done = set()
 
         def transposes(i):
@@ -368,18 +391,24 @@ def tile_qca_operator_deep_pa_t_kernel(tc, x_cat, w1, out):
             return new
 
         for i in range(-3, nch + 3):
-            at(i + 1, patch_sums)
-            at(i - 2, multiply)
-            new = at(i + 3, transposes)
-            if i == -2:
-                prepare_w()
-            at(i + 1, repeat_scalar)
-            at(i - 2, exps)
-            for b, pair, ps in new:
-                copy_pair(b, pair, ps)
+            e = extra.get(i, [])
             q = at(i - 1, quant_ops)
             m = at(i - 3, max_ops)
-            queue = at(i - 3, clamp_ops) + at(i, repeat_vector) + q[:1] + m[:1] + q[1:] + m[1:] + extra.get(i, [])
-            for op in queue:
-                op()
+            run(at(i, repeat_vector))
+            run(q[:1])
+            run(at(i - 3, clamp_ops))
+            run(q[1:])
+            run(m)
             at(i - 3, store)
+            at(i + 1, patch_sums)
+            if q:
+                multiply(i - 1, 0)
+                multiply(i - 1, 1)
+            new = at(i + 3, transposes)
+            at(i + 1, repeat_scalar)
+            at(i - 1, exps)
+            for b, pair, ps in new:
+                copy_pair(b, pair, ps)
+            if i == -3:
+                prepare_w()
+            run(e)

@@ -28,7 +28,7 @@ SC = 16
 RT = 10
 PE_ROWS = 1 + RT * STEP
 XN_ROWS = (RT - 1) * STEP + PR + 2
-HEAD_ROWS = 24
+HEAD_ROWS = 14
 
 V0 = PE_ROWS
 VR = HH - PE_ROWS
@@ -42,6 +42,8 @@ def tile_qca_operator_deep_pa_t_kernel(tc, x_cat, w1, out):
     with ExitStack() as ctx:
         const = ctx.enter_context(tc.tile_pool(name="const", bufs=1))
         work = ctx.enter_context(tc.tile_pool(name="work", bufs=4))
+        ees = ctx.enter_context(tc.tile_pool(name="ees", bufs=6))
+        pairs = ctx.enter_context(tc.tile_pool(name="pairs", bufs=2))
         xpool = ctx.enter_context(tc.tile_pool(name="xpool", bufs=6))
         psum = ctx.enter_context(tc.psum_pool(name="psum", bufs=4))
         psn = ctx.enter_context(tc.psum_pool(name="psn", bufs=2))
@@ -64,8 +66,8 @@ def tile_qca_operator_deep_pa_t_kernel(tc, x_cat, w1, out):
 
         w_sb = const.tile([P, 1024], BF16, name="w_sb")
         load_nat(0, 0, HEAD_ROWS)
-        nc.scalar.dma_start(out=w_sb, in_=w1)
         load_bot(0)
+        nc.sync.dma_start(out=w_sb, in_=w1)
         load_nat(0, HEAD_ROWS, XN_ROWS)
         load_bot(1)
         for b in range(1, B):
@@ -104,16 +106,22 @@ def tile_qca_operator_deep_pa_t_kernel(tc, x_cat, w1, out):
         w_codes = const.tile([P, 2 * P], U32, name="w_codes", align_bytes=64)
         w_scl = const.tile([P, 2 * P], U8, name="w_scl", align_bytes=64)
 
-        def prepare_w():
+        wst = {}
+
+        def sort_w():
             for q in range(4):
                 nc.vector.tensor_copy(
                     out=w_q[:, :, 32 * q : 32 * q + 32].rearrange("o r (m w) -> o r m w", m=16, w=2),
                     in_=w_sb[:, 256 * q : 256 * q + 256].rearrange("o (w m r) -> o r m w", w=2, m=16, r=8),
                 )
-            w_t = pst.tile([P, 8, P], BF16, name="xt_ps")
+
+        def transpose_w():
+            wst["t"] = pst.tile([P, 8, P], BF16, name="xt_ps")
             for r in range(8):
-                nc.tensor.transpose(w_t[:, r, :], w_q[:, r, :], ident)
-            nc.scalar.copy(out=w_g, in_=w_t.rearrange("p (g t) o -> p g o t", g=2, t=4))
+                nc.tensor.transpose(wst["t"][:, r, :], w_q[:, r, :], ident)
+
+        def regroup_w():
+            nc.scalar.copy(out=w_g, in_=wst["t"].rearrange("p (g t) o -> p g o t", g=2, t=4))
 
         def quantise_w():
             nc.vector.quantize_mx(
@@ -123,10 +131,12 @@ def tile_qca_operator_deep_pa_t_kernel(tc, x_cat, w1, out):
         strips = {}
         xts = {}
 
-        def strip_ops(b, r0, r1):
+        def strips_of(b):
             if b not in strips:
-                strips[b] = work.tile([P, 4, XN_ROWS * PC], BF16, name="strips")
+                strips[b] = pairs.tile([P, 4, XN_ROWS * PC], BF16, name="strips")
+            return strips[b]
 
+        def strip_ops(b, r0, r1):
             def one(s):
                 src = x_nat[b].rearrange("p (y x) -> p y x", x=WW)
                 views = []
@@ -135,7 +145,7 @@ def tile_qca_operator_deep_pa_t_kernel(tc, x_cat, w1, out):
 
                 def go(k):
                     return lambda: nc.vector.tensor_copy(
-                        out=strips[b][:, s + k, r0 * PC : r1 * PC].rearrange("p (y x) -> p y x", x=PC), in_=views[k]
+                        out=strips_of(b)[:, s + k, r0 * PC : r1 * PC].rearrange("p (y x) -> p y x", x=PC), in_=views[k]
                     )
 
                 return [go(0), go(1)]
@@ -156,18 +166,22 @@ def tile_qca_operator_deep_pa_t_kernel(tc, x_cat, w1, out):
             xts[b, pair] = xt
 
         plan = [
-            [(0, 0, 8), (8, 0, 0), (14, 0, 2), (14, 0, 2), (15, 0, 1)],
-            [(13, 0, 3), (13, 0, 3), (13, 0, 3), (12, 0, 4)],
-            [(13, 0, 3), (13, 0, 3), (13, 0, 3), (12, 0, 4)],
-            [(13, 0, 3), (13, 0, 3), (13, 0, 3), (4, 0, 4), (4, 0, 0), (4, 0, 0)],
+            [(0, 0, 8, 0, 0), (6, 0, 2, 0, 0), (15, 2, 1, 0, 0), (15, 2, 1, 0, 0), (15, 2, 1, 0, 0)],
+            [(11, 0, 5, 0, 0), (15, 0, 1, 0, 0), (10, 0, 6, 0, 0), (15, 0, 1, 0, 0)],
+            [(11, 0, 5, 0, 0), (15, 0, 1, 0, 0), (10, 0, 6, 0, 0), (15, 0, 1, 0, 0)],
+            [(15, 0, 1, 0, 0), (15, 0, 1, 0, 0), (10, 0, 6, 0, 1), (6, 0, 2, 0, 1), (3, 0, 1, 0, 1), (2, 0, 2, 0, 1)],
         ]
         chunks = []
         share = []
+        vshare = []
+        relu = []
         for b in range(B):
             pa, va = 0, V0
-            for np_, nr, nv in plan[b]:
+            for np_, nr, nv, ns, rl in plan[b]:
                 chunks.append((b, pa, pa + np_, va, va + nv))
                 share.append(nr * WW)
+                vshare.append(ns * WW)
+                relu.append(rl)
                 pa += np_
                 va += nv
         nch = len(chunks)
@@ -222,21 +236,25 @@ def tile_qca_operator_deep_pa_t_kernel(tc, x_cat, w1, out):
             n = VR * WW
             vc = vcs[b % 2].rearrange("p (r c) -> p r c", c=PITCH)
             flat = vcs[b % 2]
-            vo = work.tile([P, VR * WW], F32, name="vo")
-            rr = work.tile([P, VR * WW], F32, name="rr")
+            tiles = {}
+
+            def t(name):
+                if name not in tiles:
+                    tiles[name] = pairs.tile([P, VR * WW], F32, name=name)
+                return tiles[name]
 
             def shifted(off):
                 return flat[:, off : off + VR * PITCH].rearrange("p (r c) -> p r c", c=PITCH)[:, :, 0:WW]
 
             return [
                 lambda: nc.vector.tensor_tensor(
-                    out=vo, in0=x_bot[b][:, 0:n], in1=x_bot[b][:, 2 * WW : 2 * WW + n], op=ADD
+                    out=t("vo"), in0=x_bot[b][:, 0:n], in1=x_bot[b][:, 2 * WW : 2 * WW + n], op=ADD
                 ),
                 lambda: nc.vector.tensor_tensor(
-                    out=shifted(4), in0=rowsof(vo), in1=rowsof(x_bot[b][:, WW : WW + n]), op=ADD
+                    out=shifted(4), in0=rowsof(t("vo")), in1=rowsof(x_bot[b][:, WW : WW + n]), op=ADD
                 ),
-                lambda: nc.vector.tensor_tensor(out=rowsof(rr), in0=shifted(3), in1=shifted(5), op=ADD),
-                lambda: nc.vector.tensor_tensor(out=nbv[b], in0=rr, in1=vo, op=ADD),
+                lambda: nc.vector.tensor_tensor(out=rowsof(t("rr")), in0=shifted(3), in1=shifted(5), op=ADD),
+                lambda: nc.vector.tensor_tensor(out=nbv[b], in0=t("rr"), in1=t("vo"), op=ADD),
             ]
 
         def rep_tile(i):
@@ -255,12 +273,21 @@ def tile_qca_operator_deep_pa_t_kernel(tc, x_cat, w1, out):
                     out=rep_tile(i)[:, : 4 * n].rearrange("p (n t) -> p n t", t=4),
                     in_=st[i]["nb"][:, :n].unsqueeze(2).to_broadcast([P, n, 4]),
                 )
+            n = vshare[i]
+            if n:
+                b, y0, y1, va, vb = chunks[i]
+                a = (va - V0) * WW
+                n0 = pe_count(i)
+                nc.scalar.copy(
+                    out=rep_tile(i)[:, 4 * n0 : 4 * (n0 + n)].rearrange("p (n t) -> p n t", t=4),
+                    in_=nbv[b][:, a : a + n].unsqueeze(2).to_broadcast([P, n, 4]),
+                )
 
         def repeat_vector(i):
             b, y0, y1, va, vb = chunks[i]
             n0 = pe_count(i)
-            n = (vb - va) * WW
-            a = (va - V0) * WW
+            n = (vb - va) * WW - vshare[i]
+            a = (va - V0) * WW + vshare[i]
             rep = rep_tile(i)
 
             def one(src, at_, n):
@@ -273,7 +300,7 @@ def tile_qca_operator_deep_pa_t_kernel(tc, x_cat, w1, out):
             if share[i]:
                 ops.append(one(st[i]["nbs"][:, : share[i]], n0 - share[i], share[i]))
             if n:
-                ops.append(one(nbv[b][:, a : a + n], n0, n))
+                ops.append(one(nbv[b][:, a : a + n], n0 + vshare[i], n))
             return ops
 
         def quant_ops(i):
@@ -315,14 +342,21 @@ def tile_qca_operator_deep_pa_t_kernel(tc, x_cat, w1, out):
                 )
 
         def exps(i):
-            ee = work.tile([P, NPX], F32, name="ee")
+            ee = ees.tile([P, NPX], F32, name="ee")
+            if relu[i]:
+                oo = pairs.tile([P, NPX], F32, name="oo")
+                st[i]["oo"] = oo
             for k, (c0, w) in enumerate(spans(i)):
                 nc.scalar.activation(out=ee[:, c0 : c0 + w], in_=st[i]["accs"][k][:, :w], func=ACT.Exp)
+                if relu[i]:
+                    nc.scalar.activation(out=oo[:, c0 : c0 + w], in_=st[i]["accs"][k][:, :w], func=ACT.Relu)
             st[i]["ee"] = ee
 
         def clamp_ops(i):
             n = px_count(i)
             ee = st[i]["ee"]
+            if relu[i]:
+                return []
             return [
                 lambda: nc.vector.tensor_scalar(
                     out=ee[:, :n], in0=ee[:, :n], scalar1=1.0, scalar2=-1.0, op0=MIN, op1=ADD
@@ -331,6 +365,13 @@ def tile_qca_operator_deep_pa_t_kernel(tc, x_cat, w1, out):
 
         def max_ops(i):
             ee = st[i]["ee"]
+            if relu[i]:
+                n = px_count(i)
+                return [
+                    lambda: nc.vector.scalar_tensor_tensor(
+                        out=ee[:, :n], in0=ee[:, :n], scalar=-1.0, in1=st[i]["oo"][:, :n], op0=ADD, op1=MIN
+                    )
+                ]
 
             def one(k, c0, w):
                 return lambda: nc.vector.tensor_tensor(
@@ -359,8 +400,8 @@ def tile_qca_operator_deep_pa_t_kernel(tc, x_cat, w1, out):
         for op in strip_ops(0, 0, HEAD_ROWS):
             op()
         adds = [add_ops(b) for b in range(B)]
-        put(-3, strip_ops(0, HEAD_ROWS, XN_ROWS))
-        put(-2, adds[0][:2])
+        put(-3, adds[0][:2])
+        put(-2, strip_ops(0, HEAD_ROWS, XN_ROWS))
         put(-1, adds[0][2:])
         put(-1, [quantise_w])
         for k in range(4):
@@ -394,6 +435,8 @@ def tile_qca_operator_deep_pa_t_kernel(tc, x_cat, w1, out):
             e = extra.get(i, [])
             q = at(i - 1, quant_ops)
             m = at(i - 3, max_ops)
+            if i == -3:
+                sort_w()
             run(at(i, repeat_vector))
             run(q[:1])
             run(at(i - 3, clamp_ops))
@@ -409,6 +452,7 @@ def tile_qca_operator_deep_pa_t_kernel(tc, x_cat, w1, out):
             at(i - 1, exps)
             for b, pair, ps in new:
                 copy_pair(b, pair, ps)
-            if i == -3:
-                prepare_w()
+            if i == -2:
+                transpose_w()
+                regroup_w()
             run(e)

@@ -59,21 +59,23 @@ def tile_qca_operator_deep_pa_t_kernel(tc, x_cat, w1, out):
                 in_=x_cat[b].rearrange("c y x -> c (y x)")[:, r0 * WW : r1 * WW],
             )
 
-        def load_bot(b):
-            xv = x_cat[b].rearrange("(q w m) y x -> w q m (y x)", q=4, w=2, m=16)
-            for w in range(2):
-                nc.sync.dma_start(out=x_bot[b][w:P:2, 0 : (VR + 1) * WW], in_=xv[w][:, :, (V0 - 1) * WW : PIX])
+        def load_bot(b, queues):
+            xv = x_cat[b].rearrange("(q w m) y x -> q m w (y x)", q=4, w=2, m=16)
+            for q in range(4):
+                queues[q % len(queues)].dma_start(
+                    out=x_bot[b][32 * q : 32 * q + 32, 0 : (VR + 1) * WW], in_=xv[q][:, :, (V0 - 1) * WW : PIX]
+                )
 
         w_sb = const.tile([P, 1024], BF16, name="w_sb")
         load_nat(0, 0, HEAD_ROWS)
-        load_bot(0)
-        nc.sync.dma_start(out=w_sb, in_=w1)
+        load_bot(0, [nc.sync, nc.scalar])
+        nc.scalar.dma_start(out=w_sb, in_=w1)
         load_nat(0, HEAD_ROWS, XN_ROWS)
-        load_bot(1)
+        load_bot(1, [nc.sync])
         for b in range(1, B):
             load_nat(b, 0, XN_ROWS)
             if b > 1:
-                load_bot(b)
+                load_bot(b, [nc.sync])
 
         ident = const.tile([P, P], BF16, name="ident")
         make_identity(nc, ident)
@@ -166,10 +168,10 @@ def tile_qca_operator_deep_pa_t_kernel(tc, x_cat, w1, out):
             xts[b, pair] = xt
 
         plan = [
-            [(0, 0, 8, 0, 0), (6, 0, 2, 0, 0), (15, 2, 1, 0, 0), (15, 2, 1, 0, 0), (15, 2, 1, 0, 0)],
+            [(0, 0, 8, 0, 0), (6, 0, 2, 0, 0), (15, 0, 1, 0, 0), (15, 0, 1, 0, 0), (15, 0, 1, 0, 0)],
             [(11, 0, 5, 0, 0), (15, 0, 1, 0, 0), (10, 0, 6, 0, 0), (15, 0, 1, 0, 0)],
             [(11, 0, 5, 0, 0), (15, 0, 1, 0, 0), (10, 0, 6, 0, 0), (15, 0, 1, 0, 0)],
-            [(15, 0, 1, 0, 0), (15, 0, 1, 0, 0), (10, 0, 6, 0, 1), (6, 0, 2, 0, 1), (3, 0, 1, 0, 1), (2, 0, 2, 0, 1)],
+            [(15, 0, 1, 0, 0), (15, 0, 1, 0, 0), (10, 0, 6, 0, 1), (6, 0, 2, 0, 1), (5, 0, 3, 0, 1)],
         ]
         chunks = []
         share = []
@@ -435,7 +437,7 @@ def tile_qca_operator_deep_pa_t_kernel(tc, x_cat, w1, out):
             e = extra.get(i, [])
             q = at(i - 1, quant_ops)
             m = at(i - 3, max_ops)
-            if i == -3:
+            if i == -2:
                 sort_w()
             run(at(i, repeat_vector))
             run(q[:1])

@@ -28,7 +28,7 @@ SC = 16
 RT = 10
 PE_ROWS = 1 + RT * STEP
 XN_ROWS = (RT - 1) * STEP + PR + 2
-HEAD_ROWS = 14
+HEAD_ROWS = 24
 
 V0 = PE_ROWS
 VR = HH - PE_ROWS
@@ -85,23 +85,23 @@ def tile_qca_operator_deep_pa_t_kernel(tc, x_cat, w1, out):
         for k in range(2):
             nc.vector.memset(vcs[k].rearrange("p (r c) -> p r c", c=PITCH)[:, :, 0:4], 0.0)
         idp = const.tile([P, PR + 2, PC + 2], BF16, name="idp")
-        nc.vector.memset(idp, 0.0)
+        nc.gpsimd.memset(idp, 0.0)
         perm = const.tile([P, P], BF16, name="perm")
-        nc.vector.tensor_copy(
+        nc.gpsimd.tensor_copy(
             out=perm.rearrange("k (q m w) -> k q m w", q=4, m=16, w=2),
             in_=ident.rearrange("k (q w m) -> k q m w", q=4, w=2, m=16),
         )
-        nc.vector.tensor_copy(
+        nc.gpsimd.tensor_copy(
             out=idp[:, 1 : PR + 1, 1 : PC + 1], in_=ident[:, : PR * PC].rearrange("p (r c) -> p r c", c=PC)
         )
         nv1 = const.tile([P, PR, PC + 2], BF16, name="nv1")
         nv2 = const.tile([P, PR, PC + 2], BF16, name="nv2")
         nh = const.tile([P, PR, PC], BF16, name="nh")
         nmat = const.tile([P, PR, PC], BF16, name="nmat")
-        nc.vector.tensor_tensor(out=nv1, in0=idp[:, 0:PR, :], in1=idp[:, 2 : PR + 2, :], op=ADD)
-        nc.vector.tensor_tensor(out=nv2, in0=nv1, in1=idp[:, 1 : PR + 1, :], op=ADD)
-        nc.vector.tensor_tensor(out=nh, in0=nv2[:, :, 0:PC], in1=nv2[:, :, 2 : PC + 2], op=ADD)
-        nc.vector.tensor_tensor(out=nmat, in0=nh, in1=nv1[:, :, 1 : PC + 1], op=ADD)
+        nc.gpsimd.tensor_tensor(out=nv1, in0=idp[:, 0:PR, :], in1=idp[:, 2 : PR + 2, :], op=ADD)
+        nc.gpsimd.tensor_tensor(out=nv2, in0=nv1, in1=idp[:, 1 : PR + 1, :], op=ADD)
+        nc.gpsimd.tensor_tensor(out=nh, in0=nv2[:, :, 0:PC], in1=nv2[:, :, 2 : PC + 2], op=ADD)
+        nc.gpsimd.tensor_tensor(out=nmat, in0=nh, in1=nv1[:, :, 1 : PC + 1], op=ADD)
 
         w_q = const.tile([P, 8, P], BF16, name="w_q")
         w_g = const.tile([P, 2, P, 4], BF16, name="w_g", align_bytes=64)
@@ -171,7 +171,7 @@ def tile_qca_operator_deep_pa_t_kernel(tc, x_cat, w1, out):
             [(0, 0, 8, 0, 0), (6, 0, 2, 0, 0), (15, 0, 1, 0, 0), (15, 0, 1, 0, 0), (15, 0, 1, 0, 0)],
             [(11, 0, 5, 0, 0), (15, 0, 1, 0, 0), (10, 0, 6, 0, 0), (15, 0, 1, 0, 0)],
             [(11, 0, 5, 0, 0), (15, 0, 1, 0, 0), (10, 0, 6, 0, 0), (15, 0, 1, 0, 0)],
-            [(15, 0, 1, 0, 0), (15, 0, 1, 0, 0), (10, 0, 6, 0, 1), (6, 0, 2, 0, 1), (5, 0, 3, 0, 1)],
+            [(15, 0, 1, 0, 0), (15, 0, 1, 0, 1), (10, 0, 6, 0, 1), (6, 0, 2, 0, 1), (5, 0, 3, 0, 1)],
         ]
         chunks = []
         share = []
@@ -437,7 +437,7 @@ def tile_qca_operator_deep_pa_t_kernel(tc, x_cat, w1, out):
             e = extra.get(i, [])
             q = at(i - 1, quant_ops)
             m = at(i - 3, max_ops)
-            if i == -2:
+            if i == -3:
                 sort_w()
             run(at(i, repeat_vector))
             run(q[:1])

@@ -103,7 +103,9 @@ def tile_qca_operator_deep_pa_t_kernel(tc, x_cat, w1, out):
         nc.gpsimd.tensor_tensor(out=nh, in0=nv2[:, :, 0:PC], in1=nv2[:, :, 2 : PC + 2], op=ADD)
         nc.gpsimd.tensor_tensor(out=nmat, in0=nh, in1=nv1[:, :, 1 : PC + 1], op=ADD)
 
-        w_q = const.tile([P, 8, P], BF16, name="w_q")
+        identf = const.tile([P, P], F32, name="identf")
+        make_identity(nc, identf)
+        w_q = const.tile([P, 4, P], F32, name="w_q")
         w_g = const.tile([P, 2, P, 4], BF16, name="w_g", align_bytes=64)
         w_codes = const.tile([P, 2 * P], U32, name="w_codes", align_bytes=64)
         w_scl = const.tile([P, 2 * P], U8, name="w_scl", align_bytes=64)
@@ -113,17 +115,20 @@ def tile_qca_operator_deep_pa_t_kernel(tc, x_cat, w1, out):
         def sort_w():
             for q in range(4):
                 nc.vector.tensor_copy(
-                    out=w_q[:, :, 32 * q : 32 * q + 32].rearrange("o r (m w) -> o r m w", m=16, w=2),
-                    in_=w_sb[:, 256 * q : 256 * q + 256].rearrange("o (w m r) -> o r m w", w=2, m=16, r=8),
+                    out=w_q[:, :, 32 * q : 32 * q + 32].rearrange("o j (m w) -> o j m w", m=16, w=2),
+                    in_=w_sb[:, 256 * q : 256 * q + 256].bitcast(F32).rearrange("o (w m j) -> o j m w", w=2, m=16, j=4),
                 )
 
         def transpose_w():
-            wst["t"] = pst.tile([P, 8, P], BF16, name="xt_ps")
-            for r in range(8):
-                nc.tensor.transpose(wst["t"][:, r, :], w_q[:, r, :], ident)
+            wst["t"] = pst.tile([P, 4, P], F32, name="xt_ps")
+            for j in range(4):
+                nc.tensor.transpose(wst["t"][:, j, :], w_q[:, j, :], identf)
 
         def regroup_w():
-            nc.scalar.copy(out=w_g, in_=wst["t"].rearrange("p (g t) o -> p g o t", g=2, t=4))
+            nc.scalar.copy(
+                out=w_g.rearrange("p g o t -> p (g o t)").bitcast(F32).rearrange("p (g o u) -> p g o u", g=2, u=2),
+                in_=wst["t"].rearrange("p (g u) o -> p g o u", g=2, u=2),
+            )
 
         def quantise_w():
             nc.vector.quantize_mx(
@@ -168,7 +173,7 @@ def tile_qca_operator_deep_pa_t_kernel(tc, x_cat, w1, out):
             xts[b, pair] = xt
 
         plan = [
-            [(0, 0, 8, 0, 0), (6, 0, 2, 0, 0), (15, 0, 1, 0, 0), (15, 0, 1, 0, 0), (15, 0, 1, 0, 0)],
+            [(6, 0, 10, 0, 0), (15, 0, 1, 0, 0), (15, 0, 1, 0, 0), (15, 0, 1, 0, 0)],
             [(11, 0, 5, 0, 0), (15, 0, 1, 0, 0), (10, 0, 6, 0, 0), (15, 0, 1, 0, 0)],
             [(11, 0, 5, 0, 0), (15, 0, 1, 0, 0), (10, 0, 6, 0, 0), (15, 0, 1, 0, 0)],
             [(15, 0, 1, 0, 0), (15, 0, 1, 0, 1), (10, 0, 6, 0, 1), (6, 0, 2, 0, 1), (5, 0, 3, 0, 1)],

@@ -19,7 +19,8 @@ HH = 64
 WW = 64
 PIX = HH * WW
 NPX = 1024
-NT = 512
+NH = NPX // 2
+NG = 4
 
 PR, PC = 7, 18
 STEP = PR - 2
@@ -41,56 +42,41 @@ def tile_qca_operator_deep_pa_t_kernel(tc, x_cat, w1, out):
     nc = tc.nc
     with ExitStack() as ctx:
         const = ctx.enter_context(tc.tile_pool(name="const", bufs=1))
-        work = ctx.enter_context(tc.tile_pool(name="work", bufs=4))
+        work = ctx.enter_context(tc.tile_pool(name="work", bufs=3))
         ees = ctx.enter_context(tc.tile_pool(name="ees", bufs=6))
         pairs = ctx.enter_context(tc.tile_pool(name="pairs", bufs=2))
-        xpool = ctx.enter_context(tc.tile_pool(name="xpool", bufs=6))
+        xpool = ctx.enter_context(tc.tile_pool(name="xpool", bufs=8))
         psum = ctx.enter_context(tc.psum_pool(name="psum", bufs=4))
-        psn = ctx.enter_context(tc.psum_pool(name="psn", bufs=2))
+        psn = ctx.enter_context(tc.psum_pool(name="psn", bufs=1))
         pst = ctx.enter_context(tc.psum_pool(name="pst", bufs=2))
+        psr = ctx.enter_context(tc.psum_pool(name="psr", bufs=1))
         ctx.enter_context(tc.manual_schedule())
 
-        x_nat = [const.tile([P, XN_ROWS * WW], BF16, name="xn%d" % b) for b in range(B)]
-        x_bot = [const.tile([P, (VR + 2) * WW], BF16, name="xb%d" % b) for b in range(B)]
+        x_sb = [const.tile([P, (HH + 2) * WW], BF16, name="x%d" % b) for b in range(B)]
 
-        def load_nat(b, r0, r1):
-            nc.sync.dma_start(
-                out=x_nat[b][:, r0 * WW : r1 * WW],
+        def load(queue, b, r0, r1):
+            queue.dma_start(
+                out=x_sb[b][:, r0 * WW : r1 * WW],
                 in_=x_cat[b].rearrange("c y x -> c (y x)")[:, r0 * WW : r1 * WW],
             )
 
-        def load_bot(b, queues):
-            xv = x_cat[b].rearrange("(q w m) y x -> q m w (y x)", q=4, w=2, m=16)
-            for q in range(4):
-                queues[q % len(queues)].dma_start(
-                    out=x_bot[b][32 * q : 32 * q + 32, 0 : (VR + 1) * WW], in_=xv[q][:, :, (V0 - 1) * WW : PIX]
-                )
-
         w_sb = const.tile([P, 1024], BF16, name="w_sb")
-        load_nat(0, 0, HEAD_ROWS)
-        load_bot(0, [nc.sync, nc.scalar])
+        load(nc.sync, 0, 0, HEAD_ROWS)
+        load(nc.scalar, 0, V0 - 1, HH)
         nc.scalar.dma_start(out=w_sb, in_=w1)
-        load_nat(0, HEAD_ROWS, XN_ROWS)
-        load_bot(1, [nc.sync])
+        load(nc.sync, 0, HEAD_ROWS, V0 - 1)
         for b in range(1, B):
-            load_nat(b, 0, XN_ROWS)
-            if b > 1:
-                load_bot(b, [nc.sync])
+            load(nc.sync, b, 0, HH)
 
         ident = const.tile([P, P], BF16, name="ident")
         make_identity(nc, ident)
         for b in range(B):
-            nc.vector.memset(x_bot[b][:, (VR + 1) * WW :], 0.0)
+            nc.vector.memset(x_sb[b][:, HH * WW : (HH + 1) * WW], 0.0)
         vcs = [const.tile([P, (VR + 1) * PITCH], F32, name="vc%d" % k) for k in range(2)]
         for k in range(2):
             nc.vector.memset(vcs[k].rearrange("p (r c) -> p r c", c=PITCH)[:, :, 0:4], 0.0)
         idp = const.tile([P, PR + 2, PC + 2], BF16, name="idp")
         nc.gpsimd.memset(idp, 0.0)
-        perm = const.tile([P, P], BF16, name="perm")
-        nc.gpsimd.tensor_copy(
-            out=perm.rearrange("k (q m w) -> k q m w", q=4, m=16, w=2),
-            in_=ident.rearrange("k (q w m) -> k q m w", q=4, w=2, m=16),
-        )
         nc.gpsimd.tensor_copy(
             out=idp[:, 1 : PR + 1, 1 : PC + 1], in_=ident[:, : PR * PC].rearrange("p (r c) -> p r c", c=PC)
         )
@@ -102,38 +88,52 @@ def tile_qca_operator_deep_pa_t_kernel(tc, x_cat, w1, out):
         nc.gpsimd.tensor_tensor(out=nv2, in0=nv1, in1=idp[:, 1 : PR + 1, :], op=ADD)
         nc.gpsimd.tensor_tensor(out=nh, in0=nv2[:, :, 0:PC], in1=nv2[:, :, 2 : PC + 2], op=ADD)
         nc.gpsimd.tensor_tensor(out=nmat, in0=nh, in1=nv1[:, :, 1 : PC + 1], op=ADD)
-
+        perm = const.tile([P, P], BF16, name="perm")
+        for e in range(2):
+            half = slice(64 * e, 64 * e + 64)
+            nc.gpsimd.tensor_copy(
+                out=perm[:, half].rearrange("k (i a b) -> k i a b", i=4, a=4, b=4),
+                in_=ident[:, half].rearrange("k (a i b) -> k i a b", i=4, a=4, b=4),
+            )
         identf = const.tile([P, P], F32, name="identf")
         make_identity(nc, identf)
-        w_q = const.tile([P, 4, P], F32, name="w_q")
-        w_g = const.tile([P, 2, P, 4], BF16, name="w_g", align_bytes=64)
-        w_codes = const.tile([P, 2 * P], U32, name="w_codes", align_bytes=64)
-        w_scl = const.tile([P, 2 * P], U8, name="w_scl", align_bytes=64)
 
-        wst = {}
+        w_t = const.tile([P, 8, P], BF16, name="w_t")
+        w_p = const.tile([P, 8, 2, P], BF16, name="w_p")
+        w_g = const.tile([P, NG, P, 4], BF16, name="w_g", align_bytes=64)
+        w_codes = [const.tile([P, NG * P], U32, name="w_codes%d" % h, align_bytes=64) for h in range(2)]
+        w_scl = [const.tile([P, NG * P], U8, name="w_scl%d" % h, align_bytes=64) for h in range(2)]
 
-        def sort_w():
-            for q in range(4):
-                nc.vector.tensor_copy(
-                    out=w_q[:, :, 32 * q : 32 * q + 32].rearrange("o j (m w) -> o j m w", m=16, w=2),
-                    in_=w_sb[:, 256 * q : 256 * q + 256].bitcast(F32).rearrange("o (w m j) -> o j m w", w=2, m=16, j=4),
+        def w_stage_a():
+            ps = pst.tile([P, 8, P], BF16, name="xt_ps")
+            for r in range(8):
+                nc.tensor.transpose(ps[:, r, :], w_sb[:, r : 1024 : 8], ident)
+            nc.scalar.copy(out=w_t, in_=ps)
+
+        def w_stage_b():
+            ps = pst.tile([P, 8, P], BF16, name="xt_ps")
+            for r in range(8):
+                nc.tensor.transpose(ps[:, r, :], w_t[:, r, :], perm)
+            nc.scalar.copy(out=w_p, in_=ps.unsqueeze(2).to_broadcast([P, 8, 2, P]))
+
+        def w_stage_c(k):
+            ps = pst.tile([P, 4, P], F32, name="xt_ps")
+            for r in range(4):
+                nc.tensor.transpose(
+                    ps[:, r, :], w_p[:, 4 * k + r].rearrange("p d c -> p (d c)").bitcast(F32), identf
                 )
-
-        def transpose_w():
-            wst["t"] = pst.tile([P, 4, P], F32, name="xt_ps")
-            for j in range(4):
-                nc.tensor.transpose(wst["t"][:, j, :], w_q[:, j, :], identf)
-
-        def regroup_w():
             nc.scalar.copy(
-                out=w_g.rearrange("p g o t -> p (g o t)").bitcast(F32).rearrange("p (g o u) -> p g o u", g=2, u=2),
-                in_=wst["t"].rearrange("p (g u) o -> p g o u", g=2, u=2),
+                out=w_g[:, 2 * k : 2 * k + 2].rearrange("p g o t -> p (g o t)").bitcast(F32).rearrange("p (g o u) -> p g o u", g=2, u=2),
+                in_=ps.rearrange("p (g u) o -> p g o u", g=2, u=2),
             )
 
-        def quantise_w():
+        def quantise_w(h):
             nc.vector.quantize_mx(
-                out=w_codes.bitcast(FP8X4), scales=w_scl, in_=w_g.rearrange("p g o t -> p (g o t)")
+                out=w_codes[h].bitcast(FP8X4), scales=w_scl[h], in_=w_g.rearrange("p g o t -> p (g o t)")
             )
+
+        def clear_w(h):
+            nc.vector.memset(w_codes[h][64 * (1 - h) : 64 * (1 - h) + 64, :], 0)
 
         strips = {}
         xts = {}
@@ -144,27 +144,22 @@ def tile_qca_operator_deep_pa_t_kernel(tc, x_cat, w1, out):
             return strips[b]
 
         def strip_ops(b, r0, r1):
-            def one(s):
-                src = x_nat[b].rearrange("p (y x) -> p y x", x=WW)
-                views = []
-                for k in (s, s + 1):
-                    views.append(src[:, r0:r1, COL0[k] : COL0[k] + PC])
+            def go(s):
+                dst = strips_of(b).rearrange("p (a k) n -> p a k n", k=2)[:, :, s, r0 * PC : r1 * PC]
+                src = x_sb[b][:, r0 * WW + COL0[s] : r1 * WW + COL0[s]].rearrange("p (y x) -> p y x", x=WW)[:, :, 0:62]
+                nc.vector.tensor_copy(
+                    out=dst.rearrange("p a (y x) -> p a y x", x=PC),
+                    in_=src.rearrange("p y (a x) -> p a y x", a=2)[:, :, :, 0:PC],
+                )
 
-                def go(k):
-                    return lambda: nc.vector.tensor_copy(
-                        out=strips_of(b)[:, s + k, r0 * PC : r1 * PC].rearrange("p (y x) -> p y x", x=PC), in_=views[k]
-                    )
-
-                return [go(0), go(1)]
-
-            return one(0) + one(2)
+            return [lambda: go(0), lambda: go(1)]
 
         def transpose_pair(b, pair):
             ps = pst.tile([P, 8, P], BF16, name="xt_ps")
             for k in range(2):
                 r0 = (2 * pair + k) * STEP
                 for s in range(4):
-                    nc.tensor.transpose(ps[:, 4 * k + s, :], strips[b][:, s, r0 * PC : r0 * PC + P], perm)
+                    nc.tensor.transpose(ps[:, 4 * k + s, :], strips[b][:, s, r0 * PC : r0 * PC + P], ident)
             return ps
 
         def copy_pair(b, pair, ps):
@@ -173,21 +168,17 @@ def tile_qca_operator_deep_pa_t_kernel(tc, x_cat, w1, out):
             xts[b, pair] = xt
 
         plan = [
-            [(6, 0, 10, 0, 0), (15, 0, 1, 0, 0), (15, 0, 1, 0, 0), (15, 0, 1, 0, 0)],
-            [(11, 0, 5, 0, 0), (15, 0, 1, 0, 0), (10, 0, 6, 0, 0), (15, 0, 1, 0, 0)],
-            [(11, 0, 5, 0, 0), (15, 0, 1, 0, 0), (10, 0, 6, 0, 0), (15, 0, 1, 0, 0)],
-            [(15, 0, 1, 0, 0), (15, 0, 1, 0, 1), (10, 0, 6, 0, 1), (6, 0, 2, 0, 1), (5, 0, 3, 0, 1)],
+            [(6, 10, 0), (15, 1, 0), (15, 1, 0), (15, 1, 0)],
+            [(16, 0, 0), (10, 6, 1), (10, 6, 0), (15, 1, 1)],
+            [(16, 0, 0), (10, 6, 1), (10, 6, 0), (15, 1, 1)],
+            [(16, 0, 0), (10, 6, 1), (10, 6, 1), (8, 0, 1), (7, 1, 1)],
         ]
         chunks = []
-        share = []
-        vshare = []
         relu = []
         for b in range(B):
             pa, va = 0, V0
-            for np_, nr, nv, ns, rl in plan[b]:
+            for np_, nv, rl in plan[b]:
                 chunks.append((b, pa, pa + np_, va, va + nv))
-                share.append(nr * WW)
-                vshare.append(ns * WW)
                 relu.append(rl)
                 pa += np_
                 va += nv
@@ -202,6 +193,9 @@ def tile_qca_operator_deep_pa_t_kernel(tc, x_cat, w1, out):
         def px_count(i):
             return pe_count(i) + (chunks[i][4] - chunks[i][3]) * WW
 
+        def half(i):
+            return px_count(i) // 2
+
         def pairs_of(i):
             b, y0, y1, va, vb = chunks[i]
             if y1 <= y0:
@@ -212,9 +206,6 @@ def tile_qca_operator_deep_pa_t_kernel(tc, x_cat, w1, out):
 
         def patch_sums(i):
             b, y0, y1, va, vb = chunks[i]
-            n = pe_count(i)
-            if n == 0:
-                return
             nb = psn.tile([P, NPX], BF16, name="nb")
             st[i]["nb"] = nb
             nb3 = nb.rearrange("p (y x) -> p y x", x=WW)
@@ -234,6 +225,12 @@ def tile_qca_operator_deep_pa_t_kernel(tc, x_cat, w1, out):
                         stop=True,
                     )
 
+        def copy_sums(i):
+            nbs = work.tile([P, NPX], BF16, name="nbs")
+            st[i]["nbs"] = nbs
+            n = pe_count(i)
+            nc.scalar.copy(out=nbs[:, :n], in_=st[i]["nb"][:, :n])
+
         nbv = [const.tile([P, VR * WW], BF16, name="nbv%d" % b) for b in range(B)]
 
         def rowsof(ap):
@@ -241,8 +238,10 @@ def tile_qca_operator_deep_pa_t_kernel(tc, x_cat, w1, out):
 
         def add_ops(b):
             n = VR * WW
-            vc = vcs[b % 2].rearrange("p (r c) -> p r c", c=PITCH)
             flat = vcs[b % 2]
+            up = x_sb[b][:, (V0 - 1) * WW : (V0 - 1) * WW + n]
+            mid = x_sb[b][:, V0 * WW : V0 * WW + n]
+            down = x_sb[b][:, (V0 + 1) * WW : (V0 + 1) * WW + n]
             tiles = {}
 
             def t(name):
@@ -254,66 +253,57 @@ def tile_qca_operator_deep_pa_t_kernel(tc, x_cat, w1, out):
                 return flat[:, off : off + VR * PITCH].rearrange("p (r c) -> p r c", c=PITCH)[:, :, 0:WW]
 
             return [
-                lambda: nc.vector.tensor_tensor(
-                    out=t("vo"), in0=x_bot[b][:, 0:n], in1=x_bot[b][:, 2 * WW : 2 * WW + n], op=ADD
-                ),
-                lambda: nc.vector.tensor_tensor(
-                    out=shifted(4), in0=rowsof(t("vo")), in1=rowsof(x_bot[b][:, WW : WW + n]), op=ADD
-                ),
+                lambda: nc.vector.tensor_tensor(out=t("vo"), in0=up, in1=down, op=ADD),
+                lambda: nc.vector.tensor_tensor(out=shifted(4), in0=rowsof(t("vo")), in1=rowsof(mid), op=ADD),
                 lambda: nc.vector.tensor_tensor(out=rowsof(t("rr")), in0=shifted(3), in1=shifted(5), op=ADD),
                 lambda: nc.vector.tensor_tensor(out=nbv[b], in0=t("rr"), in1=t("vo"), op=ADD),
             ]
 
-        def rep_tile(i):
-            if "rep" not in st[i]:
-                st[i]["rep"] = work.tile([P, 4 * NPX], BF16, name="rep", align_bytes=64)
-            return st[i]["rep"]
-
-        def repeat_scalar(i):
-            n = pe_count(i) - share[i]
-            if share[i]:
-                nbs = work.tile([P, NPX], BF16, name="nbs")
-                nc.scalar.copy(out=nbs[:, : share[i]], in_=st[i]["nb"][:, n : n + share[i]])
-                st[i]["nbs"] = nbs
-            if n:
-                nc.scalar.copy(
-                    out=rep_tile(i)[:, : 4 * n].rearrange("p (n t) -> p n t", t=4),
-                    in_=st[i]["nb"][:, :n].unsqueeze(2).to_broadcast([P, n, 4]),
-                )
-            n = vshare[i]
-            if n:
-                b, y0, y1, va, vb = chunks[i]
-                a = (va - V0) * WW
-                n0 = pe_count(i)
-                nc.scalar.copy(
-                    out=rep_tile(i)[:, 4 * n0 : 4 * (n0 + n)].rearrange("p (n t) -> p n t", t=4),
-                    in_=nbv[b][:, a : a + n].unsqueeze(2).to_broadcast([P, n, 4]),
-                )
-
-        def repeat_vector(i):
+        def seam_ops(i):
             b, y0, y1, va, vb = chunks[i]
-            n0 = pe_count(i)
-            n = (vb - va) * WW - vshare[i]
-            a = (va - V0) * WW + vshare[i]
-            rep = rep_tile(i)
+            n = pe_count(i)
+            if n % P == 0 or va == vb:
+                return []
+            a = (va - V0) * WW
+            return [lambda: nc.vector.tensor_copy(out=st[i]["nbs"][:, n : n + WW], in_=nbv[b][:, a : a + WW])]
 
-            def one(src, at_, n):
-                return lambda: nc.vector.tensor_copy(
-                    out=rep[:, 4 * at_ : 4 * (at_ + n)].rearrange("p (n t) -> p n t", t=4),
-                    in_=src.unsqueeze(2).to_broadcast([P, n, 4]),
+        def blocks_to_rows(i):
+            b, y0, y1, va, vb = chunks[i]
+            n = pe_count(i)
+            nj = half(i) // P
+            ps = pst.tile([P, 4, 2, P], BF16, name="xt_ps")
+            for h in range(2):
+                for j in range(nj):
+                    a = h * half(i) + j * P
+                    if a < n:
+                        src = st[i]["nbs"][:, a : a + P]
+                    else:
+                        v = (va - V0) * WW + a - n
+                        src = nbv[b][:, v : v + P]
+                    nc.tensor.transpose(ps[:, j, h, :], src, perm)
+            rows = work.tile([P, 4, 2, P], BF16, name="rows")
+            st[i]["rows"] = rows
+            nc.scalar.copy(out=rows[:, :nj], in_=ps[:, :nj])
+
+        def rows_to_pairs(i):
+            nj = half(i) // P
+            ps = psr.tile([P, NH], F32, name="pp")
+            for j in range(nj):
+                nc.tensor.transpose(
+                    ps[:, j * P : (j + 1) * P], st[i]["rows"][:, j].rearrange("p h c -> p (h c)").bitcast(F32), identf
                 )
-
-            ops = []
-            if share[i]:
-                ops.append(one(st[i]["nbs"][:, : share[i]], n0 - share[i], share[i]))
-            if n:
-                ops.append(one(nbv[b][:, a : a + n], n0 + vshare[i], n))
-            return ops
+            n = half(i)
+            rep = work.tile([P, 4 * NH], BF16, name="rep", align_bytes=64)
+            st[i]["rep"] = rep
+            nc.scalar.copy(
+                out=rep[:, : 4 * n].bitcast(F32).rearrange("p (n t) -> p n t", t=2),
+                in_=ps[:, :n].unsqueeze(2).to_broadcast([P, n, 2]),
+            )
 
         def quant_ops(i):
-            n = px_count(i)
-            codes = work.tile([P, 2, NPX], U32, name="codes", align_bytes=64)
-            scl = work.tile([P, 2, NPX], U8, name="scl", align_bytes=64)
+            n = half(i)
+            codes = work.tile([P, NG, NH], U32, name="codes", align_bytes=64)
+            scl = work.tile([P, NG, NH], U8, name="scl", align_bytes=64)
             st[i]["codes"] = codes
             st[i]["scl"] = scl
             rep = st[i]["rep"]
@@ -323,40 +313,39 @@ def tile_qca_operator_deep_pa_t_kernel(tc, x_cat, w1, out):
                     out=codes[:, g, :n].bitcast(FP8X4), scales=scl[:, g, :n], in_=rep[:, : 4 * n]
                 )
 
-            return [one(0), one(1)]
+            return [one(g) for g in range(NG)]
 
-        def spans(i):
-            n = px_count(i)
-            return [(c0, min(NT, n - c0)) for c0 in range(0, n, NT)]
-
-        def multiply(i, g):
+        def multiply(i):
             codes = st[i]["codes"]
             scl = st[i]["scl"]
-            if g == 0:
-                st[i]["accs"] = []
-            for k, (c0, w) in enumerate(spans(i)):
-                if g == 0:
-                    acc = psum.tile([P, NT], F32, name="acc")
-                    st[i]["accs"].append(acc)
-                nc.tensor.matmul_mx(
-                    out=st[i]["accs"][k][:, :w],
-                    lhsT=w_codes[:, g * P : (g + 1) * P].bitcast(FP8X4),
-                    lhsT_scale=w_scl[:, g * P : (g + 1) * P],
-                    rhs=codes[:, g, c0 : c0 + w].bitcast(FP8X4),
-                    rhs_scale=scl[:, g, c0 : c0 + w],
-                    start=(g == 0),
-                    stop=(g == 1),
-                )
+            n = half(i)
+            accs = []
+            for h in range(2):
+                acc = psum.tile([P, NH], F32, name="acc")
+                accs.append(acc)
+            st[i]["accs"] = accs
+            for g in range(NG):
+                for h in range(2):
+                    nc.tensor.matmul_mx(
+                        out=accs[h][:, :n],
+                        lhsT=w_codes[h][:, g * P : (g + 1) * P].bitcast(FP8X4),
+                        lhsT_scale=w_scl[h][:, g * P : (g + 1) * P],
+                        rhs=codes[:, g, :n].bitcast(FP8X4),
+                        rhs_scale=scl[:, g, :n],
+                        start=(g == 0),
+                        stop=(g == NG - 1),
+                    )
 
         def exps(i):
+            n = half(i)
             ee = ees.tile([P, NPX], F32, name="ee")
             if relu[i]:
                 oo = pairs.tile([P, NPX], F32, name="oo")
                 st[i]["oo"] = oo
-            for k, (c0, w) in enumerate(spans(i)):
-                nc.scalar.activation(out=ee[:, c0 : c0 + w], in_=st[i]["accs"][k][:, :w], func=ACT.Exp)
+            for h in range(2):
+                nc.scalar.activation(out=ee[:, h * n : (h + 1) * n], in_=st[i]["accs"][h][:, :n], func=ACT.Exp)
                 if relu[i]:
-                    nc.scalar.activation(out=oo[:, c0 : c0 + w], in_=st[i]["accs"][k][:, :w], func=ACT.Relu)
+                    nc.scalar.activation(out=oo[:, h * n : (h + 1) * n], in_=st[i]["accs"][h][:, :n], func=ACT.Relu)
             st[i]["ee"] = ee
 
         def clamp_ops(i):
@@ -379,13 +368,14 @@ def tile_qca_operator_deep_pa_t_kernel(tc, x_cat, w1, out):
                         out=ee[:, :n], in0=ee[:, :n], scalar=-1.0, in1=st[i]["oo"][:, :n], op0=ADD, op1=MIN
                     )
                 ]
+            n = half(i)
 
-            def one(k, c0, w):
+            def one(h):
                 return lambda: nc.vector.tensor_tensor(
-                    out=ee[:, c0 : c0 + w], in0=ee[:, c0 : c0 + w], in1=st[i]["accs"][k][:, :w], op=MAX
+                    out=ee[:, h * n : (h + 1) * n], in0=ee[:, h * n : (h + 1) * n], in1=st[i]["accs"][h][:, :n], op=MAX
                 )
 
-            return [one(k, c0, w) for k, (c0, w) in enumerate(spans(i))]
+            return [one(0), one(1)]
 
         def store(i):
             b, y0, y1, va, vb = chunks[i]
@@ -407,18 +397,18 @@ def tile_qca_operator_deep_pa_t_kernel(tc, x_cat, w1, out):
         for op in strip_ops(0, 0, HEAD_ROWS):
             op()
         adds = [add_ops(b) for b in range(B)]
-        put(-3, adds[0][:2])
-        put(-2, strip_ops(0, HEAD_ROWS, XN_ROWS))
-        put(-1, adds[0][2:])
-        put(-1, [quantise_w])
-        for k in range(4):
-            put(k, [adds[1][k]])
-        for b in range(1, B):
+        put(-5, adds[0][:2])
+        put(-4, strip_ops(0, HEAD_ROWS, XN_ROWS))
+        put(-3, adds[0][2:])
+        put(0, [lambda: quantise_w(0), lambda: quantise_w(1), lambda: clear_w(0), lambda: clear_w(1)])
+        put(-2, adds[1][:2])
+        put(-2, strip_ops(1, 0, XN_ROWS))
+        put(-1, adds[1][2:])
+        for b in range(2, B):
             for k, op in enumerate(strip_ops(b, 0, XN_ROWS)):
-                put(first[b] - 5 + k // 2, [op])
-            if b > 1:
-                for k in range(4):
-                    put(bottom[b] - 4 + k, [adds[b][k]])
+                put(first[b] - 7 + k, [op])
+            for k in range(4):
+                put(bottom[b] - 7 + k, [adds[b][k]])
 
         def at(i, f):
             return f(i) if 0 <= i < nch else []
@@ -430,36 +420,34 @@ def tile_qca_operator_deep_pa_t_kernel(tc, x_cat, w1, out):
         done = set()
 
         def transposes(i):
-            new = []
             b = chunks[i][0]
             for pair in pairs_of(i):
                 if (b, pair) not in done:
                     done.add((b, pair))
-                    new.append((b, pair, transpose_pair(b, pair)))
-            return new
+                    copy_pair(b, pair, transpose_pair(b, pair))
 
-        for i in range(-3, nch + 3):
-            e = extra.get(i, [])
+        for i in range(-5, nch + 3):
             q = at(i - 1, quant_ops)
-            m = at(i - 3, max_ops)
-            if i == -3:
-                sort_w()
-            run(at(i, repeat_vector))
-            run(q[:1])
+            run(at(i + 2, seam_ops))
+            run(q[:2])
             run(at(i - 3, clamp_ops))
-            run(q[1:])
-            run(m)
+            run(q[2:])
+            run(at(i - 3, max_ops))
             at(i - 3, store)
-            at(i + 1, patch_sums)
+            at(i + 1, rows_to_pairs)
+            if i + 3 >= 0 and i + 3 < nch:
+                patch_sums(i + 3)
+                copy_sums(i + 3)
+            at(i + 2, blocks_to_rows)
+            at(i + 5, transposes)
             if q:
-                multiply(i - 1, 0)
-                multiply(i - 1, 1)
-            new = at(i + 3, transposes)
-            at(i + 1, repeat_scalar)
-            at(i - 1, exps)
-            for b, pair, ps in new:
-                copy_pair(b, pair, ps)
+                multiply(i - 1)
+                exps(i - 1)
+            if i == -3:
+                w_stage_a()
             if i == -2:
-                transpose_w()
-                regroup_w()
-            run(e)
+                w_stage_b()
+            if i == -1:
+                w_stage_c(0)
+                w_stage_c(1)
+            run(extra.get(i, []))

@@ -18,21 +18,20 @@ B = 4
 HH = 64
 WW = 64
 PIX = HH * WW
-NPX = 1024
-NH = NPX // 2
+NH = 512
 NG = 4
 
 PR, PC = 7, 18
 STEP = PR - 2
 COL0 = (0, 15, 31, 46)
 SC = 16
-RT = 10
-PE_ROWS = 1 + RT * STEP
-XN_ROWS = (RT - 1) * STEP + PR + 2
-HEAD_ROWS = 24
+UNITS = 5
+NS = UNITS * STEP
+XN_ROWS = 2 * NS + 3
 
-V0 = PE_ROWS
-VR = HH - PE_ROWS
+V0 = 2 * NS
+VR = HH - V0
+VH = VR // 2
 PITCH = 68
 
 FLOPS = 2 * B * PIX * 1024 * P
@@ -47,34 +46,43 @@ def tile_qca_operator_deep_pa_t_kernel(tc, x_cat, w1, out):
         pairs = ctx.enter_context(tc.tile_pool(name="pairs", bufs=2))
         xpool = ctx.enter_context(tc.tile_pool(name="xpool", bufs=8))
         psum = ctx.enter_context(tc.psum_pool(name="psum", bufs=4))
-        psn = ctx.enter_context(tc.psum_pool(name="psn", bufs=1))
+        psn = ctx.enter_context(tc.psum_pool(name="psn", bufs=2))
         pst = ctx.enter_context(tc.psum_pool(name="pst", bufs=2))
-        psr = ctx.enter_context(tc.psum_pool(name="psr", bufs=1))
         ctx.enter_context(tc.manual_schedule())
 
-        x_sb = [const.tile([P, (HH + 2) * WW], BF16, name="x%d" % b) for b in range(B)]
+        x_sb = [const.tile([P, (HH + 3) * WW], BF16, name="x%d" % b) for b in range(B)]
 
         def load(queue, b, r0, r1):
             queue.dma_start(
-                out=x_sb[b][:, r0 * WW : r1 * WW],
+                out=x_sb[b][:, (r0 + 1) * WW : (r1 + 1) * WW],
                 in_=x_cat[b].rearrange("c y x -> c (y x)")[:, r0 * WW : r1 * WW],
             )
 
         w_sb = const.tile([P, 1024], BF16, name="w_sb")
-        load(nc.sync, 0, 0, HEAD_ROWS)
-        load(nc.scalar, 0, V0 - 1, HH)
+        load(nc.sync, 0, 0, 13)
+        load(nc.scalar, 0, 24, 38)
         nc.scalar.dma_start(out=w_sb, in_=w1)
-        load(nc.sync, 0, HEAD_ROWS, V0 - 1)
+        load(nc.sync, 0, 38, HH)
+        load(nc.sync, 0, 13, 24)
         for b in range(1, B):
             load(nc.sync, b, 0, HH)
+
 
         ident = const.tile([P, P], BF16, name="ident")
         make_identity(nc, ident)
         for b in range(B):
-            nc.vector.memset(x_sb[b][:, HH * WW : (HH + 1) * WW], 0.0)
+            nc.vector.memset(x_sb[b][:, 0:WW], 0.0)
+            nc.vector.memset(x_sb[b][:, (HH + 1) * WW : (HH + 2) * WW], 0.0)
         vcs = [const.tile([P, (VR + 1) * PITCH], F32, name="vc%d" % k) for k in range(2)]
         for k in range(2):
             nc.vector.memset(vcs[k].rearrange("p (r c) -> p r c", c=PITCH)[:, :, 0:4], 0.0)
+        permx = const.tile([P, P], BF16, name="permx")
+        for u in range(2):
+            for e in range(2):
+                nc.gpsimd.tensor_copy(
+                    out=permx[:, 64 * u + 32 * e : 64 * u + 32 * e + 32].rearrange("k (i a c) -> k i a c", i=4, a=4),
+                    in_=ident[:, 64 * e : 64 * e + 64].rearrange("k (a i c v) -> k v i a c", a=4, i=4, c=2)[:, u],
+                )
         idp = const.tile([P, PR + 2, PC + 2], BF16, name="idp")
         nc.gpsimd.memset(idp, 0.0)
         nc.gpsimd.tensor_copy(
@@ -88,12 +96,12 @@ def tile_qca_operator_deep_pa_t_kernel(tc, x_cat, w1, out):
         nc.gpsimd.tensor_tensor(out=nv2, in0=nv1, in1=idp[:, 1 : PR + 1, :], op=ADD)
         nc.gpsimd.tensor_tensor(out=nh, in0=nv2[:, :, 0:PC], in1=nv2[:, :, 2 : PC + 2], op=ADD)
         nc.gpsimd.tensor_tensor(out=nmat, in0=nh, in1=nv1[:, :, 1 : PC + 1], op=ADD)
-        perm = const.tile([P, P], BF16, name="perm")
+        permw = const.tile([P, P], BF16, name="permw")
         for e in range(2):
-            half = slice(64 * e, 64 * e + 64)
+            hs = slice(64 * e, 64 * e + 64)
             nc.gpsimd.tensor_copy(
-                out=perm[:, half].rearrange("k (i a b) -> k i a b", i=4, a=4, b=4),
-                in_=ident[:, half].rearrange("k (a i b) -> k i a b", i=4, a=4, b=4),
+                out=permw[:, hs].rearrange("k (i a b) -> k i a b", i=4, a=4),
+                in_=ident[:, hs].rearrange("k (a i b) -> k i a b", a=4, i=4),
             )
         identf = const.tile([P, P], F32, name="identf")
         make_identity(nc, identf)
@@ -113,7 +121,7 @@ def tile_qca_operator_deep_pa_t_kernel(tc, x_cat, w1, out):
         def w_stage_b():
             ps = pst.tile([P, 8, P], BF16, name="xt_ps")
             for r in range(8):
-                nc.tensor.transpose(ps[:, r, :], w_t[:, r, :], perm)
+                nc.tensor.transpose(ps[:, r, :], w_t[:, r, :], permw)
             nc.scalar.copy(out=w_p, in_=ps.unsqueeze(2).to_broadcast([P, 8, 2, P]))
 
         def w_stage_c(k):
@@ -122,9 +130,9 @@ def tile_qca_operator_deep_pa_t_kernel(tc, x_cat, w1, out):
                 nc.tensor.transpose(
                     ps[:, r, :], w_p[:, 4 * k + r].rearrange("p d c -> p (d c)").bitcast(F32), identf
                 )
+            words = w_g[:, 2 * k : 2 * k + 2].rearrange("p g o t -> p (g o t)").bitcast(F32)
             nc.scalar.copy(
-                out=w_g[:, 2 * k : 2 * k + 2].rearrange("p g o t -> p (g o t)").bitcast(F32).rearrange("p (g o u) -> p g o u", g=2, u=2),
-                in_=ps.rearrange("p (g u) o -> p g o u", g=2, u=2),
+                out=words.rearrange("p (g o u) -> p g o u", g=2, u=2), in_=ps.rearrange("p (g u) o -> p g o u", g=2, u=2)
             )
 
         def quantise_w(h):
@@ -144,9 +152,11 @@ def tile_qca_operator_deep_pa_t_kernel(tc, x_cat, w1, out):
             return strips[b]
 
         def strip_ops(b, r0, r1):
+            q0, q1 = r0 + 1, r1 + 1
+
             def go(s):
-                dst = strips_of(b).rearrange("p (a k) n -> p a k n", k=2)[:, :, s, r0 * PC : r1 * PC]
-                src = x_sb[b][:, r0 * WW + COL0[s] : r1 * WW + COL0[s]].rearrange("p (y x) -> p y x", x=WW)[:, :, 0:62]
+                dst = strips_of(b).rearrange("p (a k) n -> p a k n", k=2)[:, :, s, q0 * PC : q1 * PC]
+                src = x_sb[b][:, q0 * WW + COL0[s] : q1 * WW + COL0[s]].rearrange("p (y x) -> p y x", x=WW)[:, :, 0:62]
                 nc.vector.tensor_copy(
                     out=dst.rearrange("p a (y x) -> p a y x", x=PC),
                     in_=src.rearrange("p y (a x) -> p a y x", a=2)[:, :, :, 0:PC],
@@ -154,84 +164,51 @@ def tile_qca_operator_deep_pa_t_kernel(tc, x_cat, w1, out):
 
             return [lambda: go(0), lambda: go(1)]
 
-        def transpose_pair(b, pair):
-            ps = pst.tile([P, 8, P], BF16, name="xt_ps")
-            for k in range(2):
-                r0 = (2 * pair + k) * STEP
+        def transpose_unit(b, k):
+            ps = pst.tile([P, 4, 2, 2, 64], BF16, name="xt_ps")
+            for h in range(2):
+                q0 = (NS * h + k * STEP) * PC
                 for s in range(4):
-                    nc.tensor.transpose(ps[:, 4 * k + s, :], strips[b][:, s, r0 * PC : r0 * PC + P], ident)
+                    nc.tensor.transpose(ps[:, s, :, h, :], strips[b][:, s, q0 : q0 + P], permx)
             return ps
 
-        def copy_pair(b, pair, ps):
-            xt = xpool.tile([P, 8, P], BF16, name="xt")
-            nc.scalar.copy(out=xt, in_=ps)
-            xts[b, pair] = xt
+        def copy_unit(b, k, ps):
+            xt = xpool.tile([P, 4, 2, P], BF16, name="xt")
+            nc.scalar.copy(out=xt.rearrange("p s u m -> p (s u m)"), in_=ps.rearrange("p s u h i -> p (s u h i)"))
+            xts[b, k] = xt
 
         plan = [
-            [(6, 10, 0), (15, 1, 0), (15, 1, 0), (15, 1, 0)],
-            [(16, 0, 0), (10, 6, 1), (10, 6, 0), (15, 1, 1)],
-            [(16, 0, 0), (10, 6, 1), (10, 6, 0), (15, 1, 1)],
-            [(16, 0, 0), (10, 6, 1), (10, 6, 1), (8, 0, 1), (7, 1, 1)],
+            [(4, 0, 0), (8, 0, 0), (8, 0, 0), (4, 4, 0), (1, 3, 0)],
+            [(8, 0, 1), (8, 0, 0), (4, 4, 1), (5, 3, 0)],
+            [(8, 0, 1), (8, 0, 0), (4, 4, 1), (5, 3, 0)],
+            [(8, 0, 1), (8, 0, 0), (4, 4, 1), (4, 0, 1), (1, 3, 1)],
         ]
         chunks = []
         relu = []
         for b in range(B):
-            pa, va = 0, V0
-            for np_, nv, rl in plan[b]:
-                chunks.append((b, pa, pa + np_, va, va + nv))
+            j, v = 0, 0
+            for nj, nv, rl in plan[b]:
+                chunks.append((b, j, j + nj, v, v + nv))
                 relu.append(rl)
-                pa += np_
-                va += nv
+                j += nj
+                v += nv
         nch = len(chunks)
         st = [dict() for c in chunks]
         first = [min(i for i in range(nch) if chunks[i][0] == b) for b in range(B)]
         bottom = [min(i for i in range(nch) if chunks[i][0] == b and chunks[i][4] > chunks[i][3]) for b in range(B)]
 
-        def pe_count(i):
-            return (chunks[i][2] - chunks[i][1]) * WW
-
-        def px_count(i):
-            return pe_count(i) + (chunks[i][4] - chunks[i][3]) * WW
-
         def half(i):
-            return px_count(i) // 2
+            b, j0, j1, v0, v1 = chunks[i]
+            return (j1 - j0 + v1 - v0) * WW
 
-        def pairs_of(i):
-            b, y0, y1, va, vb = chunks[i]
-            if y1 <= y0:
-                return []
-            lo = max(0, (y0 - 1) // STEP)
-            hi = max(0, (y1 - 2) // STEP)
-            return list(range(lo // 2, hi // 2 + 1))
+        def units_of(i):
+            b, j0, j1, v0, v1 = chunks[i]
+            return list(range(j0 // STEP, (j1 - 1) // STEP + 1)) if j1 > j0 else []
 
-        def patch_sums(i):
-            b, y0, y1, va, vb = chunks[i]
-            nb = psn.tile([P, NPX], BF16, name="nb")
-            st[i]["nb"] = nb
-            nb3 = nb.rearrange("p (y x) -> p y x", x=WW)
-            for rt in range(RT):
-                r0 = rt * STEP
-                ya = max(y0, r0 + 1 if rt else 0)
-                yb = min(y1, r0 + PR - 1)
-                if yb <= ya:
-                    continue
-                for s in range(4):
-                    c0 = SC * s - COL0[s]
-                    nc.tensor.matmul(
-                        out=nb3[:, ya - y0 : yb - y0, SC * s : SC * s + SC],
-                        lhsT=xts[b, rt // 2][:, 4 * (rt % 2) + s, :],
-                        rhs=nmat[:, ya - r0 : yb - r0, c0 : c0 + SC],
-                        start=True,
-                        stop=True,
-                    )
-
-        def copy_sums(i):
-            nbs = work.tile([P, NPX], BF16, name="nbs")
-            st[i]["nbs"] = nbs
-            n = pe_count(i)
-            nc.scalar.copy(out=nbs[:, :n], in_=st[i]["nb"][:, :n])
-
-        nbv = [const.tile([P, VR * WW], BF16, name="nbv%d" % b) for b in range(B)]
+        nbv = [const.tile([P, (VR + 1) * WW], BF16, name="nbv%d" % b) for b in range(B)]
+        for b in range(B):
+            nc.vector.memset(nbv[b][:, VR * WW :], 0.0)
+        vts = {}
 
         def rowsof(ap):
             return ap.rearrange("p (r c) -> p r c", c=WW)
@@ -239,9 +216,9 @@ def tile_qca_operator_deep_pa_t_kernel(tc, x_cat, w1, out):
         def add_ops(b):
             n = VR * WW
             flat = vcs[b % 2]
-            up = x_sb[b][:, (V0 - 1) * WW : (V0 - 1) * WW + n]
-            mid = x_sb[b][:, V0 * WW : V0 * WW + n]
-            down = x_sb[b][:, (V0 + 1) * WW : (V0 + 1) * WW + n]
+            up = x_sb[b][:, V0 * WW : V0 * WW + n]
+            mid = x_sb[b][:, (V0 + 1) * WW : (V0 + 1) * WW + n]
+            down = x_sb[b][:, (V0 + 2) * WW : (V0 + 2) * WW + n]
             tiles = {}
 
             def t(name):
@@ -256,48 +233,50 @@ def tile_qca_operator_deep_pa_t_kernel(tc, x_cat, w1, out):
                 lambda: nc.vector.tensor_tensor(out=t("vo"), in0=up, in1=down, op=ADD),
                 lambda: nc.vector.tensor_tensor(out=shifted(4), in0=rowsof(t("vo")), in1=rowsof(mid), op=ADD),
                 lambda: nc.vector.tensor_tensor(out=rowsof(t("rr")), in0=shifted(3), in1=shifted(5), op=ADD),
-                lambda: nc.vector.tensor_tensor(out=nbv[b], in0=t("rr"), in1=t("vo"), op=ADD),
+                lambda: nc.vector.tensor_tensor(out=nbv[b][:, 0:n], in0=t("rr"), in1=t("vo"), op=ADD),
             ]
 
-        def seam_ops(i):
-            b, y0, y1, va, vb = chunks[i]
-            n = pe_count(i)
-            if n % P == 0 or va == vb:
-                return []
-            a = (va - V0) * WW
-            return [lambda: nc.vector.tensor_copy(out=st[i]["nbs"][:, n : n + WW], in_=nbv[b][:, a : a + WW])]
-
-        def blocks_to_rows(i):
-            b, y0, y1, va, vb = chunks[i]
-            n = pe_count(i)
-            nj = half(i) // P
-            ps = pst.tile([P, 4, 2, P], BF16, name="xt_ps")
+        def turn_bottom(b):
+            ps = pst.tile([P, 4, 2, 2, 64], BF16, name="xt_ps")
             for h in range(2):
-                for j in range(nj):
-                    a = h * half(i) + j * P
-                    if a < n:
-                        src = st[i]["nbs"][:, a : a + P]
-                    else:
-                        v = (va - V0) * WW + a - n
-                        src = nbv[b][:, v : v + P]
-                    nc.tensor.transpose(ps[:, j, h, :], src, perm)
-            rows = work.tile([P, 4, 2, P], BF16, name="rows")
-            st[i]["rows"] = rows
-            nc.scalar.copy(out=rows[:, :nj], in_=ps[:, :nj])
+                for q in range(4):
+                    a = (VH * h + 2 * q) * WW
+                    nc.tensor.transpose(ps[:, q, :, h, :], nbv[b][:, a : a + P], permx)
+            vt = xpool.tile([P, 4, 2, P], BF16, name="vt", bufs=2)
+            nc.scalar.copy(out=vt.rearrange("p s u m -> p (s u m)"), in_=ps.rearrange("p s u h i -> p (s u h i)"))
+            vts[b] = vt
 
-        def rows_to_pairs(i):
-            nj = half(i) // P
-            ps = psr.tile([P, NH], F32, name="pp")
-            for j in range(nj):
-                nc.tensor.transpose(
-                    ps[:, j * P : (j + 1) * P], st[i]["rows"][:, j].rearrange("p h c -> p (h c)").bitcast(F32), identf
-                )
+        def sums(i):
+            b, j0, j1, v0, v1 = chunks[i]
+            nb = psn.tile([P, 2, NH], BF16, name="nb")
+            st[i]["nb"] = nb
+            for v in range(v0, v1, 2):
+                for u in range(2):
+                    c = (v - v0) * WW
+                    nc.tensor.transpose(nb[:, u, c : c + P], vts[b][:, v // 2, u, :], ident)
+            at_ = (v1 - v0) * WW
+            for k in units_of(i):
+                ra = max(j0, k * STEP)
+                rb = min(j1, (k + 1) * STEP)
+                for s in range(4):
+                    c0 = SC * s - COL0[s]
+                    for u in range(2):
+                        to = nb[:, u, at_ + (ra - j0) * WW : at_ + (rb - j0) * WW].rearrange("p (y x) -> p y x", x=WW)
+                        nc.tensor.matmul(
+                            out=to[:, :, SC * s : SC * s + SC],
+                            lhsT=xts[b, k][:, s, u, :],
+                            rhs=nmat[:, ra - k * STEP + 1 : rb - k * STEP + 1, c0 : c0 + SC],
+                            start=True,
+                            stop=True,
+                        )
+
+        def repeat(i):
             n = half(i)
             rep = work.tile([P, 4 * NH], BF16, name="rep", align_bytes=64)
             st[i]["rep"] = rep
             nc.scalar.copy(
-                out=rep[:, : 4 * n].bitcast(F32).rearrange("p (n t) -> p n t", t=2),
-                in_=ps[:, :n].unsqueeze(2).to_broadcast([P, n, 2]),
+                out=rep[:, : 4 * n].rearrange("p (n r u) -> p n r u", r=2, u=2),
+                in_=st[i]["nb"][:, :, :n].rearrange("p u n -> p n u").unsqueeze(2).to_broadcast([P, n, 2, 2]),
             )
 
         def quant_ops(i):
@@ -338,9 +317,9 @@ def tile_qca_operator_deep_pa_t_kernel(tc, x_cat, w1, out):
 
         def exps(i):
             n = half(i)
-            ee = ees.tile([P, NPX], F32, name="ee")
+            ee = ees.tile([P, 2 * NH], F32, name="ee")
             if relu[i]:
-                oo = pairs.tile([P, NPX], F32, name="oo")
+                oo = pairs.tile([P, 2 * NH], F32, name="oo")
                 st[i]["oo"] = oo
             for h in range(2):
                 nc.scalar.activation(out=ee[:, h * n : (h + 1) * n], in_=st[i]["accs"][h][:, :n], func=ACT.Exp)
@@ -349,7 +328,7 @@ def tile_qca_operator_deep_pa_t_kernel(tc, x_cat, w1, out):
             st[i]["ee"] = ee
 
         def clamp_ops(i):
-            n = px_count(i)
+            n = 2 * half(i)
             ee = st[i]["ee"]
             if relu[i]:
                 return []
@@ -361,14 +340,13 @@ def tile_qca_operator_deep_pa_t_kernel(tc, x_cat, w1, out):
 
         def max_ops(i):
             ee = st[i]["ee"]
+            n = half(i)
             if relu[i]:
-                n = px_count(i)
                 return [
                     lambda: nc.vector.scalar_tensor_tensor(
-                        out=ee[:, :n], in0=ee[:, :n], scalar=-1.0, in1=st[i]["oo"][:, :n], op0=ADD, op1=MIN
+                        out=ee[:, : 2 * n], in0=ee[:, : 2 * n], scalar=-1.0, in1=st[i]["oo"][:, : 2 * n], op0=ADD, op1=MIN
                     )
                 ]
-            n = half(i)
 
             def one(h):
                 return lambda: nc.vector.tensor_tensor(
@@ -378,37 +356,42 @@ def tile_qca_operator_deep_pa_t_kernel(tc, x_cat, w1, out):
             return [one(0), one(1)]
 
         def store(i):
-            b, y0, y1, va, vb = chunks[i]
-            at_ = 0
-            for ya, yb in ((y0, y1), (va, vb)):
-                n = (yb - ya) * WW
-                if n:
-                    nc.sync.dma_start(
-                        out=out[b].rearrange("o y x -> o (y x)")[:, ya * WW : yb * WW],
-                        in_=st[i]["ee"][:, at_ : at_ + n],
-                    )
-                at_ += n
+            b, j0, j1, v0, v1 = chunks[i]
+            ee = st[i]["ee"][:, : 2 * half(i)].rearrange("p (h n) -> p h n", h=2)
+            nv = (v1 - v0) * WW
+            if nv:
+                to = out[b][:, V0:HH, :].rearrange("o (h y) x -> o h (y x)", h=2)
+                nc.sync.dma_start(out=to[:, :, v0 * WW : v1 * WW], in_=ee[:, :, :nv])
+            if j1 > j0:
+                to = out[b][:, 0:V0, :].rearrange("o (h y) x -> o h (y x)", h=2)
+                nc.sync.dma_start(out=to[:, :, j0 * WW : j1 * WW], in_=ee[:, :, nv:])
 
         extra = {}
 
         def put(i, ops):
             extra.setdefault(i, []).extend(ops)
 
-        for op in strip_ops(0, 0, HEAD_ROWS):
-            op()
         adds = [add_ops(b) for b in range(B)]
-        put(-5, adds[0][:2])
-        put(-4, strip_ops(0, HEAD_ROWS, XN_ROWS))
-        put(-3, adds[0][2:])
+        for op in strip_ops(0, -1, 12) + strip_ops(0, 24, 37):
+            op()
+        put(-3, strip_ops(0, 12, 24) + strip_ops(0, 37, 52))
+        put(-3, adds[0][:2])
+        put(-2, adds[0][2:])
+        put(-1, strip_ops(1, -1, XN_ROWS - 1))
+        put(-1, adds[1][:2])
         put(0, [lambda: quantise_w(0), lambda: quantise_w(1), lambda: clear_w(0), lambda: clear_w(1)])
-        put(-2, adds[1][:2])
-        put(-2, strip_ops(1, 0, XN_ROWS))
-        put(-1, adds[1][2:])
+        for k in range(2, 4):
+            put(bottom[1] - 7 + k, [adds[1][k]])
         for b in range(2, B):
-            for k, op in enumerate(strip_ops(b, 0, XN_ROWS)):
-                put(first[b] - 7 + k, [op])
+            for k, op in enumerate(strip_ops(b, -1, XN_ROWS - 1)):
+                put(first[b] - 5 + k, [op])
             for k in range(4):
                 put(bottom[b] - 7 + k, [adds[b][k]])
+
+        turn = {}
+        for b in range(B):
+            turn.setdefault(bottom[b] - 3, []).append(b)
+        early = {-3: [w_stage_a], -2: [w_stage_b], -1: [lambda: w_stage_c(0), lambda: w_stage_c(1)]}
 
         def at(i, f):
             return f(i) if 0 <= i < nch else []
@@ -419,35 +402,28 @@ def tile_qca_operator_deep_pa_t_kernel(tc, x_cat, w1, out):
 
         done = set()
 
-        def transposes(i):
-            b = chunks[i][0]
-            for pair in pairs_of(i):
-                if (b, pair) not in done:
-                    done.add((b, pair))
-                    copy_pair(b, pair, transpose_pair(b, pair))
+        def units_to_do(i):
+            new = [(chunks[i][0], k) for k in units_of(i) if (chunks[i][0], k) not in done]
+            done.update(new)
+            return new
 
-        for i in range(-5, nch + 3):
+        for i in range(-3, nch + 3):
             q = at(i - 1, quant_ops)
-            run(at(i + 2, seam_ops))
             run(q[:2])
             run(at(i - 3, clamp_ops))
             run(q[2:])
             run(at(i - 3, max_ops))
             at(i - 3, store)
-            at(i + 1, rows_to_pairs)
-            if i + 3 >= 0 and i + 3 < nch:
-                patch_sums(i + 3)
-                copy_sums(i + 3)
-            at(i + 2, blocks_to_rows)
-            at(i + 5, transposes)
-            if q:
-                multiply(i - 1)
-                exps(i - 1)
-            if i == -3:
-                w_stage_a()
-            if i == -2:
-                w_stage_b()
-            if i == -1:
-                w_stage_c(0)
-                w_stage_c(1)
+            at(i + 1, sums)
+            at(i + 1, repeat)
+            new = at(i + 3, units_to_do)
+            for un in new[:1]:
+                copy_unit(*un, transpose_unit(*un))
+            for un in new[1:]:
+                copy_unit(*un, transpose_unit(*un))
+            for b in turn.get(i, []):
+                turn_bottom(b)
+            at(i - 1, multiply)
+            at(i - 1, exps)
+            run(early.get(i, []))
             run(extra.get(i, []))

@@ -44,9 +44,10 @@ def tile_qca_operator_deep_pa_t_kernel(tc, x_cat, w1, out):
         work = ctx.enter_context(tc.tile_pool(name="work", bufs=3))
         ees = ctx.enter_context(tc.tile_pool(name="ees", bufs=6))
         pairs = ctx.enter_context(tc.tile_pool(name="pairs", bufs=2))
+        oos = ctx.enter_context(tc.tile_pool(name="oos", bufs=2))
         xpool = ctx.enter_context(tc.tile_pool(name="xpool", bufs=8))
-        psum = ctx.enter_context(tc.psum_pool(name="psum", bufs=4))
-        psn = ctx.enter_context(tc.psum_pool(name="psn", bufs=2))
+        psum = ctx.enter_context(tc.psum_pool(name="psum", bufs=5))
+        psn = ctx.enter_context(tc.psum_pool(name="psn", bufs=1))
         pst = ctx.enter_context(tc.psum_pool(name="pst", bufs=2))
         ctx.enter_context(tc.manual_schedule())
 
@@ -107,7 +108,7 @@ def tile_qca_operator_deep_pa_t_kernel(tc, x_cat, w1, out):
         make_identity(nc, identf)
 
         w_t = const.tile([P, 8, P], BF16, name="w_t")
-        w_p = const.tile([P, 8, 2, P], BF16, name="w_p")
+        w_p = const.tile([P, 9, P], BF16, name="w_p")
         w_g = const.tile([P, NG, P, 4], BF16, name="w_g", align_bytes=64)
         w_codes = [const.tile([P, NG * P], U32, name="w_codes%d" % h, align_bytes=64) for h in range(2)]
         w_scl = [const.tile([P, NG * P], U8, name="w_scl%d" % h, align_bytes=64) for h in range(2)]
@@ -122,13 +123,14 @@ def tile_qca_operator_deep_pa_t_kernel(tc, x_cat, w1, out):
             ps = pst.tile([P, 8, P], BF16, name="xt_ps")
             for r in range(8):
                 nc.tensor.transpose(ps[:, r, :], w_t[:, r, :], permw)
-            nc.scalar.copy(out=w_p, in_=ps.unsqueeze(2).to_broadcast([P, 8, 2, P]))
+            nc.scalar.copy(out=w_p[:, 0:8], in_=ps)
+            nc.scalar.copy(out=w_p[:, 8], in_=ps[:, 0])
 
         def w_stage_c(k):
             ps = pst.tile([P, 4, P], F32, name="xt_ps")
             for r in range(4):
                 nc.tensor.transpose(
-                    ps[:, r, :], w_p[:, 4 * k + r].rearrange("p d c -> p (d c)").bitcast(F32), identf
+                    ps[:, r, :], w_p[:, 4 * k + r : 4 * k + r + 2].rearrange("p d c -> p (d c)").bitcast(F32), identf
                 )
             words = w_g[:, 2 * k : 2 * k + 2].rearrange("p g o t -> p (g o t)").bitcast(F32)
             nc.scalar.copy(
@@ -141,7 +143,7 @@ def tile_qca_operator_deep_pa_t_kernel(tc, x_cat, w1, out):
             )
 
         def clear_w(h):
-            nc.vector.memset(w_codes[h][64 * (1 - h) : 64 * (1 - h) + 64, :], 0)
+            nc.gpsimd.memset(w_codes[h][64 * (1 - h) : 64 * (1 - h) + 64, :], 0)
 
         strips = {}
         xts = {}
@@ -178,10 +180,10 @@ def tile_qca_operator_deep_pa_t_kernel(tc, x_cat, w1, out):
             xts[b, k] = xt
 
         plan = [
-            [(4, 0, 0), (8, 0, 0), (8, 0, 0), (4, 4, 0), (1, 3, 0)],
-            [(8, 0, 1), (8, 0, 0), (4, 4, 1), (5, 3, 0)],
-            [(8, 0, 1), (8, 0, 0), (4, 4, 1), (5, 3, 0)],
-            [(8, 0, 1), (8, 0, 0), (4, 4, 1), (4, 0, 1), (1, 3, 1)],
+            [(4, 0, 0), (4, 0, 0), (8, 0, 0), (8, 0, 0), (1, 7, 0)],
+            [(8, 0, 2), (8, 0, 0), (4, 4, 2), (5, 3, 0)],
+            [(8, 0, 2), (8, 0, 0), (4, 4, 2), (5, 3, 0)],
+            [(8, 0, 2), (8, 0, 0), (4, 4, 2), (4, 0, 2), (1, 3, 2)],
         ]
         chunks = []
         relu = []
@@ -318,42 +320,45 @@ def tile_qca_operator_deep_pa_t_kernel(tc, x_cat, w1, out):
         def exps(i):
             n = half(i)
             ee = ees.tile([P, 2 * NH], F32, name="ee")
-            if relu[i]:
-                oo = pairs.tile([P, 2 * NH], F32, name="oo")
-                st[i]["oo"] = oo
-            for h in range(2):
-                nc.scalar.activation(out=ee[:, h * n : (h + 1) * n], in_=st[i]["accs"][h][:, :n], func=ACT.Exp)
-                if relu[i]:
-                    nc.scalar.activation(out=oo[:, h * n : (h + 1) * n], in_=st[i]["accs"][h][:, :n], func=ACT.Relu)
             st[i]["ee"] = ee
+            if relu[i]:
+                st[i]["oo"] = oos.tile([P, 2 * NH], F32, name="oo")
+            for h in range(2):
+                acc = st[i]["accs"][h][:, :n]
+                nc.scalar.activation(out=ee[:, h * n : (h + 1) * n], in_=acc, func=ACT.Exp)
+                if h < relu[i]:
+                    nc.scalar.activation(out=st[i]["oo"][:, h * n : (h + 1) * n], in_=acc, func=ACT.Relu)
 
         def clamp_ops(i):
-            n = 2 * half(i)
+            n = half(i)
             ee = st[i]["ee"]
-            if relu[i]:
+            if relu[i] == 2:
                 return []
+            a = relu[i] * n
             return [
                 lambda: nc.vector.tensor_scalar(
-                    out=ee[:, :n], in0=ee[:, :n], scalar1=1.0, scalar2=-1.0, op0=MIN, op1=ADD
+                    out=ee[:, a : 2 * n], in0=ee[:, a : 2 * n], scalar1=1.0, scalar2=-1.0, op0=MIN, op1=ADD
                 )
             ]
 
         def max_ops(i):
             ee = st[i]["ee"]
             n = half(i)
-            if relu[i]:
-                return [
-                    lambda: nc.vector.scalar_tensor_tensor(
-                        out=ee[:, : 2 * n], in0=ee[:, : 2 * n], scalar=-1.0, in1=st[i]["oo"][:, : 2 * n], op0=ADD, op1=MIN
+            ops = []
+            for h in range(relu[i], 2):
+                ops.append(
+                    lambda h=h: nc.vector.tensor_tensor(
+                        out=ee[:, h * n : (h + 1) * n], in0=ee[:, h * n : (h + 1) * n], in1=st[i]["accs"][h][:, :n], op=MAX
                     )
-                ]
-
-            def one(h):
-                return lambda: nc.vector.tensor_tensor(
-                    out=ee[:, h * n : (h + 1) * n], in0=ee[:, h * n : (h + 1) * n], in1=st[i]["accs"][h][:, :n], op=MAX
                 )
-
-            return [one(0), one(1)]
+            if relu[i]:
+                r = relu[i] * n
+                ops.append(
+                    lambda: nc.vector.scalar_tensor_tensor(
+                        out=ee[:, :r], in0=ee[:, :r], scalar=-1.0, in1=st[i]["oo"][:, :r], op0=ADD, op1=MIN
+                    )
+                )
+            return ops
 
         def store(i):
             b, j0, j1, v0, v1 = chunks[i]

@@ -110,8 +110,8 @@ def tile_qca_operator_deep_pa_t_kernel(tc, x_cat, w1, out):
         w_t = const.tile([P, 8, P], BF16, name="w_t")
         w_p = const.tile([P, 9, P], BF16, name="w_p")
         w_g = const.tile([P, NG, P, 4], BF16, name="w_g", align_bytes=64)
-        w_codes = [const.tile([P, NG * P], U32, name="w_codes%d" % h, align_bytes=64) for h in range(2)]
-        w_scl = [const.tile([P, NG * P], U8, name="w_scl%d" % h, align_bytes=64) for h in range(2)]
+        w_codes = [const.tile([P, NG * P], U32, name="w_codes%d" % h, align_bytes=256) for h in range(2)]
+        w_scl = [const.tile([P, NG * P], U8, name="w_scl%d" % h, align_bytes=256) for h in range(2)]
 
         def w_stage_a():
             ps = pst.tile([P, 8, P], BF16, name="xt_ps")
@@ -274,7 +274,7 @@ def tile_qca_operator_deep_pa_t_kernel(tc, x_cat, w1, out):
 
         def repeat(i):
             n = half(i)
-            rep = work.tile([P, 4 * NH], BF16, name="rep", align_bytes=64)
+            rep = work.tile([P, 4 * NH], BF16, name="rep", align_bytes=256)
             st[i]["rep"] = rep
             nc.scalar.copy(
                 out=rep[:, : 4 * n].rearrange("p (n r u) -> p n r u", r=2, u=2),
@@ -283,8 +283,8 @@ def tile_qca_operator_deep_pa_t_kernel(tc, x_cat, w1, out):
 
         def quant_ops(i):
             n = half(i)
-            codes = work.tile([P, NG, NH], U32, name="codes", align_bytes=64)
-            scl = work.tile([P, NG, NH], U8, name="scl", align_bytes=64)
+            codes = work.tile([P, NG, NH], U32, name="codes", align_bytes=256)
+            scl = work.tile([P, NG, NH], U8, name="scl", align_bytes=256)
             st[i]["codes"] = codes
             st[i]["scl"] = scl
             rep = st[i]["rep"]

@@ -97,34 +97,21 @@ def tile_qca_operator_deep_pa_t_kernel(tc, x_cat, w1, out):
         nc.gpsimd.tensor_tensor(out=nv2, in0=nv1, in1=idp[:, 1 : PR + 1, :], op=ADD)
         nc.gpsimd.tensor_tensor(out=nh, in0=nv2[:, :, 0:PC], in1=nv2[:, :, 2 : PC + 2], op=ADD)
         nc.gpsimd.tensor_tensor(out=nmat, in0=nh, in1=nv1[:, :, 1 : PC + 1], op=ADD)
-        permw = const.tile([P, P], BF16, name="permw")
-        for e in range(2):
-            hs = slice(64 * e, 64 * e + 64)
-            nc.gpsimd.tensor_copy(
-                out=permw[:, hs].rearrange("k (i a b) -> k i a b", i=4, a=4),
-                in_=ident[:, hs].rearrange("k (a i b) -> k i a b", a=4, i=4),
-            )
         identf = const.tile([P, P], F32, name="identf")
         make_identity(nc, identf)
 
-        w_t = const.tile([P, 8, P], BF16, name="w_t")
         w_p = const.tile([P, 9, P], BF16, name="w_p")
         w_g = const.tile([P, NG, P, 4], BF16, name="w_g", align_bytes=64)
         w_codes = [const.tile([P, NG * P], U32, name="w_codes%d" % h, align_bytes=256) for h in range(2)]
         w_scl = [const.tile([P, NG * P], U8, name="w_scl%d" % h, align_bytes=256) for h in range(2)]
 
-        def w_stage_a():
-            ps = pst.tile([P, 8, P], BF16, name="xt_ps")
-            for r in range(8):
-                nc.tensor.transpose(ps[:, r, :], w_sb[:, r : 1024 : 8], ident)
-            nc.scalar.copy(out=w_t, in_=ps)
-
-        def w_stage_b():
-            ps = pst.tile([P, 8, P], BF16, name="xt_ps")
-            for r in range(8):
-                nc.tensor.transpose(ps[:, r, :], w_t[:, r, :], permw)
-            nc.scalar.copy(out=w_p[:, 0:8], in_=ps)
-            nc.scalar.copy(out=w_p[:, 8], in_=ps[:, 0])
+        def sort_w():
+            for e in range(2):
+                src = w_sb[:, 512 * e : 512 * e + 512].rearrange("o (a i b r) -> o i r a b", a=4, i=4, b=4)
+                dst = w_p[:, 0:8, 64 * e : 64 * e + 64].rearrange("o r (i a b) -> o i r a b", i=4, a=4)
+                for i in range(4):
+                    nc.vector.tensor_copy(out=dst[:, i], in_=src[:, i])
+            nc.vector.tensor_copy(out=w_p[:, 8], in_=w_p[:, 0])
 
         def w_stage_c(k):
             ps = pst.tile([P, 4, P], F32, name="xt_ps")
@@ -183,7 +170,7 @@ def tile_qca_operator_deep_pa_t_kernel(tc, x_cat, w1, out):
             [(4, 0, 0), (4, 0, 0), (8, 0, 0), (8, 0, 0), (1, 7, 0)],
             [(8, 0, 2), (8, 0, 0), (4, 4, 2), (5, 3, 0)],
             [(8, 0, 2), (8, 0, 0), (4, 4, 2), (5, 3, 0)],
-            [(8, 0, 2), (8, 0, 0), (4, 4, 2), (4, 0, 2), (1, 3, 2)],
+            [(8, 0, 2), (8, 0, 0), (4, 4, 2), (1, 3, 2), (4, 0, 0)],
         ]
         chunks = []
         relu = []
@@ -345,17 +332,17 @@ def tile_qca_operator_deep_pa_t_kernel(tc, x_cat, w1, out):
             ee = st[i]["ee"]
             n = half(i)
             ops = []
-            for h in range(relu[i], 2):
-                ops.append(
-                    lambda h=h: nc.vector.tensor_tensor(
-                        out=ee[:, h * n : (h + 1) * n], in0=ee[:, h * n : (h + 1) * n], in1=st[i]["accs"][h][:, :n], op=MAX
-                    )
-                )
             if relu[i]:
                 r = relu[i] * n
                 ops.append(
                     lambda: nc.vector.scalar_tensor_tensor(
                         out=ee[:, :r], in0=ee[:, :r], scalar=-1.0, in1=st[i]["oo"][:, :r], op0=ADD, op1=MIN
+                    )
+                )
+            for h in range(relu[i], 2):
+                ops.append(
+                    lambda h=h: nc.vector.tensor_tensor(
+                        out=ee[:, h * n : (h + 1) * n], in0=ee[:, h * n : (h + 1) * n], in1=st[i]["accs"][h][:, :n], op=MAX
                     )
                 )
             return ops
@@ -379,13 +366,14 @@ def tile_qca_operator_deep_pa_t_kernel(tc, x_cat, w1, out):
         adds = [add_ops(b) for b in range(B)]
         for op in strip_ops(0, -1, 12) + strip_ops(0, 24, 37):
             op()
+        sort_w()
         put(-3, strip_ops(0, 12, 24) + strip_ops(0, 37, 52))
         put(-3, adds[0][:2])
         put(-2, adds[0][2:])
         put(-1, strip_ops(1, -1, XN_ROWS - 1))
-        put(-1, adds[1][:2])
+        put(-1, adds[1][:1])
         put(0, [lambda: quantise_w(0), lambda: quantise_w(1), lambda: clear_w(0), lambda: clear_w(1)])
-        for k in range(2, 4):
+        for k in range(1, 4):
             put(bottom[1] - 7 + k, [adds[1][k]])
         for b in range(2, B):
             for k, op in enumerate(strip_ops(b, -1, XN_ROWS - 1)):
@@ -396,7 +384,7 @@ def tile_qca_operator_deep_pa_t_kernel(tc, x_cat, w1, out):
         turn = {}
         for b in range(B):
             turn.setdefault(bottom[b] - 3, []).append(b)
-        early = {-3: [w_stage_a], -2: [w_stage_b], -1: [lambda: w_stage_c(0), lambda: w_stage_c(1)]}
+        early = {-2: [lambda: w_stage_c(0), lambda: w_stage_c(1)]}
 
         def at(i, f):
             return f(i) if 0 <= i < nch else []

@@ -107,10 +107,10 @@ def tile_qca_operator_deep_pa_t_kernel(tc, x_cat, w1, out):
 
         def sort_w():
             for e in range(2):
-                src = w_sb[:, 512 * e : 512 * e + 512].rearrange("o (a i b r) -> o i r a b", a=4, i=4, b=4)
-                dst = w_p[:, 0:8, 64 * e : 64 * e + 64].rearrange("o r (i a b) -> o i r a b", i=4, a=4)
-                for i in range(4):
-                    nc.vector.tensor_copy(out=dst[:, i], in_=src[:, i])
+                nc.vector.tensor_copy(
+                    out=w_p[:, 0:8, 64 * e : 64 * e + 64].rearrange("o r (i a b) -> o r i a b", i=4, a=4),
+                    in_=w_sb[:, 512 * e : 512 * e + 512].rearrange("o (a i b r) -> o r i a b", a=4, i=4, b=4),
+                )
             nc.vector.tensor_copy(out=w_p[:, 8], in_=w_p[:, 0])
 
         def w_stage_c(k):
@@ -367,19 +367,20 @@ def tile_qca_operator_deep_pa_t_kernel(tc, x_cat, w1, out):
         for op in strip_ops(0, -1, 12) + strip_ops(0, 24, 37):
             op()
         sort_w()
-        put(-3, strip_ops(0, 12, 24) + strip_ops(0, 37, 52))
-        put(-3, adds[0][:2])
-        put(-2, adds[0][2:])
-        put(-1, strip_ops(1, -1, XN_ROWS - 1))
+        s0 = strip_ops(0, 12, 24) + strip_ops(0, 37, 52)
+        s1 = strip_ops(1, -1, XN_ROWS - 1)
+        put(-3, [s0[0], s0[2], adds[0][0], s0[1], s0[3], adds[0][1]])
+        put(-2, [s1[0], adds[0][2], s1[1], adds[0][3]])
         put(-1, adds[1][:1])
         put(0, [lambda: quantise_w(0), lambda: quantise_w(1), lambda: clear_w(0), lambda: clear_w(1)])
         for k in range(1, 4):
             put(bottom[1] - 7 + k, [adds[1][k]])
-        for b in range(2, B):
+        for b in range(2, 4):
             for k, op in enumerate(strip_ops(b, -1, XN_ROWS - 1)):
                 put(first[b] - 5 + k, [op])
+        for b in (2, 3):
             for k in range(4):
-                put(bottom[b] - 7 + k, [adds[b][k]])
+                put(bottom[b] - 7 + k * 1, [adds[b][k]])
 
         turn = {}
         for b in range(B):

@@ -7,6 +7,7 @@ FP8X4 = mybir.dt.float8_e4m3fn_x4
 BF16 = mybir.dt.bfloat16
 F32 = mybir.dt.float32
 U32 = mybir.dt.uint32
+I32 = mybir.dt.int32
 U8 = mybir.dt.uint8
 ADD = mybir.AluOpType.add
 MIN = mybir.AluOpType.min
@@ -51,7 +52,8 @@ def tile_qca_operator_deep_pa_t_kernel(tc, x_cat, w1, out):
         pst = ctx.enter_context(tc.psum_pool(name="pst", bufs=2))
         ctx.enter_context(tc.manual_schedule())
 
-        x_sb = [const.tile([P, (HH + 3) * WW], BF16, name="x%d" % b) for b in range(B)]
+        x_all = const.tile([P, B, (HH + 3) * WW], BF16, name="x_all")
+        x_sb = [x_all[:, b] for b in range(B)]
 
         def load(queue, b, r0, r1):
             queue.dma_start(
@@ -71,47 +73,48 @@ def tile_qca_operator_deep_pa_t_kernel(tc, x_cat, w1, out):
 
         ident = const.tile([P, P], BF16, name="ident")
         make_identity(nc, ident)
-        for b in range(B):
-            nc.vector.memset(x_sb[b][:, 0:WW], 0.0)
-            nc.vector.memset(x_sb[b][:, (HH + 1) * WW : (HH + 2) * WW], 0.0)
-        vcs = [const.tile([P, (VR + 1) * PITCH], F32, name="vc%d" % k) for k in range(2)]
-        for k in range(2):
-            nc.vector.memset(vcs[k].rearrange("p (r c) -> p r c", c=PITCH)[:, :, 0:4], 0.0)
-        permx = const.tile([P, P], BF16, name="permx")
-        for u in range(2):
-            for e in range(2):
-                nc.gpsimd.tensor_copy(
-                    out=permx[:, 64 * u + 32 * e : 64 * u + 32 * e + 32].rearrange("k (i a c) -> k i a c", i=4, a=4),
-                    in_=ident[:, 64 * e : 64 * e + 64].rearrange("k (a i c v) -> k v i a c", a=4, i=4, c=2)[:, u],
-                )
+        identf = const.tile([P, P], F32, name="identf")
+        make_identity(nc, identf)
+        nc.vector.memset(x_all[:, :, 0:WW], 0.0)
         idp = const.tile([P, PR + 2, PC + 2], BF16, name="idp")
-        nc.gpsimd.memset(idp, 0.0)
-        nc.gpsimd.tensor_copy(
-            out=idp[:, 1 : PR + 1, 1 : PC + 1], in_=ident[:, : PR * PC].rearrange("p (r c) -> p r c", c=PC)
-        )
+        nc.vector.memset(idp, 0.0)
+        permx = const.tile([P, P], BF16, name="permx")
+
+        def permute(u, e):
+            nc.vector.tensor_copy(
+                out=permx[:, 64 * u + 32 * e : 64 * u + 32 * e + 32].rearrange("k (i a c) -> k i a c", i=4, a=4),
+                in_=ident[:, 64 * e : 64 * e + 64].rearrange("k (a i c v) -> k v i a c", a=4, i=4, c=2)[:, u],
+            )
+
         nv1 = const.tile([P, PR, PC + 2], BF16, name="nv1")
         nv2 = const.tile([P, PR, PC + 2], BF16, name="nv2")
         nh = const.tile([P, PR, PC], BF16, name="nh")
         nmat = const.tile([P, PR, PC], BF16, name="nmat")
-        nc.gpsimd.tensor_tensor(out=nv1, in0=idp[:, 0:PR, :], in1=idp[:, 2 : PR + 2, :], op=ADD)
-        nc.gpsimd.tensor_tensor(out=nv2, in0=nv1, in1=idp[:, 1 : PR + 1, :], op=ADD)
-        nc.gpsimd.tensor_tensor(out=nh, in0=nv2[:, :, 0:PC], in1=nv2[:, :, 2 : PC + 2], op=ADD)
-        nc.gpsimd.tensor_tensor(out=nmat, in0=nh, in1=nv1[:, :, 1 : PC + 1], op=ADD)
-        identf = const.tile([P, P], F32, name="identf")
-        make_identity(nc, identf)
+        permute(0, 0)
+        nc.vector.tensor_copy(
+            out=idp[:, 1 : PR + 1, 1 : PC + 1], in_=ident[:, : PR * PC].rearrange("p (r c) -> p r c", c=PC)
+        )
+        permute(0, 1)
+        nc.vector.tensor_tensor(out=nv1, in0=idp[:, 0:PR, :], in1=idp[:, 2 : PR + 2, :], op=ADD)
+        permute(1, 0)
+        nc.vector.tensor_tensor(out=nv2, in0=nv1, in1=idp[:, 1 : PR + 1, :], op=ADD)
+        permute(1, 1)
+        vcs = const.tile([P, 2, (VR + 1) * PITCH], F32, name="vcs")
+        nbv = const.tile([P, B, (VR + 1) * WW], BF16, name="nbv")
 
         w_p = const.tile([P, 9, P], BF16, name="w_p")
         w_g = const.tile([P, NG, P, 4], BF16, name="w_g", align_bytes=64)
         w_codes = [const.tile([P, NG * P], U32, name="w_codes%d" % h, align_bytes=256) for h in range(2)]
-        w_scl = [const.tile([P, NG * P], U8, name="w_scl%d" % h, align_bytes=256) for h in range(2)]
+        w_all = const.tile([P, NG * P], U32, name="w_all", align_bytes=256)
+        w_scl = const.tile([P, NG * P], U8, name="w_scl", align_bytes=256)
+        for h in range(2):
+            nc.gpsimd.memset(w_codes[h], 0)
 
-        def sort_w():
-            for e in range(2):
-                nc.vector.tensor_copy(
-                    out=w_p[:, 0:8, 64 * e : 64 * e + 64].rearrange("o r (i a b) -> o r i a b", i=4, a=4),
-                    in_=w_sb[:, 512 * e : 512 * e + 512].rearrange("o (a i b r) -> o r i a b", a=4, i=4, b=4),
-                )
-            nc.vector.tensor_copy(out=w_p[:, 8], in_=w_p[:, 0])
+        def sort_w(e):
+            nc.vector.tensor_copy(
+                out=w_p[:, 0:8, 64 * e : 64 * e + 64].rearrange("o r (i a b) -> o r i a b", i=4, a=4),
+                in_=w_sb[:, 512 * e : 512 * e + 512].rearrange("o (a i b r) -> o r i a b", a=4, i=4, b=4),
+            )
 
         def w_stage_c(k):
             ps = pst.tile([P, 4, P], F32, name="xt_ps")
@@ -124,13 +127,13 @@ def tile_qca_operator_deep_pa_t_kernel(tc, x_cat, w1, out):
                 out=words.rearrange("p (g o u) -> p g o u", g=2, u=2), in_=ps.rearrange("p (g u) o -> p g o u", g=2, u=2)
             )
 
-        def quantise_w(h):
+        def quantise_w():
             nc.vector.quantize_mx(
-                out=w_codes[h].bitcast(FP8X4), scales=w_scl[h], in_=w_g.rearrange("p g o t -> p (g o t)")
+                out=w_all.bitcast(FP8X4), scales=w_scl, in_=w_g.rearrange("p g o t -> p (g o t)")
             )
-
-        def clear_w(h):
-            nc.gpsimd.memset(w_codes[h][64 * (1 - h) : 64 * (1 - h) + 64, :], 0)
+            for h in range(2):
+                part = slice(64 * h, 64 * h + 64)
+                nc.sync.dma_start(out=w_codes[h][part, :].bitcast(I32), in_=w_all[part, :].bitcast(I32))
 
         strips = {}
         xts = {}
@@ -170,7 +173,7 @@ def tile_qca_operator_deep_pa_t_kernel(tc, x_cat, w1, out):
             [(4, 0, 0), (4, 0, 0), (8, 0, 0), (8, 0, 0), (1, 7, 0)],
             [(8, 0, 2), (8, 0, 0), (4, 4, 2), (5, 3, 0)],
             [(8, 0, 2), (8, 0, 0), (4, 4, 2), (5, 3, 0)],
-            [(8, 0, 2), (8, 0, 0), (4, 4, 2), (1, 3, 2), (4, 0, 0)],
+            [(8, 0, 2), (8, 0, 1), (4, 4, 2), (1, 3, 2), (4, 0, 0)],
         ]
         chunks = []
         relu = []
@@ -194,9 +197,6 @@ def tile_qca_operator_deep_pa_t_kernel(tc, x_cat, w1, out):
             b, j0, j1, v0, v1 = chunks[i]
             return list(range(j0 // STEP, (j1 - 1) // STEP + 1)) if j1 > j0 else []
 
-        nbv = [const.tile([P, (VR + 1) * WW], BF16, name="nbv%d" % b) for b in range(B)]
-        for b in range(B):
-            nc.vector.memset(nbv[b][:, VR * WW :], 0.0)
         vts = {}
 
         def rowsof(ap):
@@ -204,7 +204,7 @@ def tile_qca_operator_deep_pa_t_kernel(tc, x_cat, w1, out):
 
         def add_ops(b):
             n = VR * WW
-            flat = vcs[b % 2]
+            flat = vcs[:, b % 2]
             up = x_sb[b][:, V0 * WW : V0 * WW + n]
             mid = x_sb[b][:, (V0 + 1) * WW : (V0 + 1) * WW + n]
             down = x_sb[b][:, (V0 + 2) * WW : (V0 + 2) * WW + n]
@@ -222,7 +222,7 @@ def tile_qca_operator_deep_pa_t_kernel(tc, x_cat, w1, out):
                 lambda: nc.vector.tensor_tensor(out=t("vo"), in0=up, in1=down, op=ADD),
                 lambda: nc.vector.tensor_tensor(out=shifted(4), in0=rowsof(t("vo")), in1=rowsof(mid), op=ADD),
                 lambda: nc.vector.tensor_tensor(out=rowsof(t("rr")), in0=shifted(3), in1=shifted(5), op=ADD),
-                lambda: nc.vector.tensor_tensor(out=nbv[b][:, 0:n], in0=t("rr"), in1=t("vo"), op=ADD),
+                lambda: nc.vector.tensor_tensor(out=nbv[:, b, 0:n], in0=t("rr"), in1=t("vo"), op=ADD),
             ]
 
         def turn_bottom(b):
@@ -230,7 +230,7 @@ def tile_qca_operator_deep_pa_t_kernel(tc, x_cat, w1, out):
             for h in range(2):
                 for q in range(4):
                     a = (VH * h + 2 * q) * WW
-                    nc.tensor.transpose(ps[:, q, :, h, :], nbv[b][:, a : a + P], permx)
+                    nc.tensor.transpose(ps[:, q, :, h, :], nbv[:, b, a : a + P], permx)
             vt = xpool.tile([P, 4, 2, P], BF16, name="vt", bufs=2)
             nc.scalar.copy(out=vt.rearrange("p s u m -> p (s u m)"), in_=ps.rearrange("p s u h i -> p (s u h i)"))
             vts[b] = vt
@@ -297,7 +297,7 @@ def tile_qca_operator_deep_pa_t_kernel(tc, x_cat, w1, out):
                     nc.tensor.matmul_mx(
                         out=accs[h][:, :n],
                         lhsT=w_codes[h][:, g * P : (g + 1) * P].bitcast(FP8X4),
-                        lhsT_scale=w_scl[h][:, g * P : (g + 1) * P],
+                        lhsT_scale=w_scl[:, g * P : (g + 1) * P],
                         rhs=codes[:, g, :n].bitcast(FP8X4),
                         rhs_scale=scl[:, g, :n],
                         start=(g == 0),
@@ -366,13 +366,20 @@ def tile_qca_operator_deep_pa_t_kernel(tc, x_cat, w1, out):
         adds = [add_ops(b) for b in range(B)]
         for op in strip_ops(0, -1, 12) + strip_ops(0, 24, 37):
             op()
-        sort_w()
+        nc.vector.memset(x_all[:, :, (HH + 1) * WW : (HH + 2) * WW], 0.0)
+        nc.vector.tensor_tensor(out=nh, in0=nv2[:, :, 0:PC], in1=nv2[:, :, 2 : PC + 2], op=ADD)
+        sort_w(0)
+        nc.vector.tensor_tensor(out=nmat, in0=nh, in1=nv1[:, :, 1 : PC + 1], op=ADD)
+        sort_w(1)
+        nc.vector.memset(vcs.rearrange("p m (r c) -> p (m r) c", c=PITCH)[:, :, 0:4], 0.0)
+        nc.vector.memset(nbv[:, :, VR * WW :], 0.0)
+        nc.vector.tensor_copy(out=w_p[:, 8], in_=w_p[:, 0])
         s0 = strip_ops(0, 12, 24) + strip_ops(0, 37, 52)
         s1 = strip_ops(1, -1, XN_ROWS - 1)
         put(-3, [s0[0], s0[2], adds[0][0], s0[1], s0[3], adds[0][1]])
         put(-2, [s1[0], adds[0][2], s1[1], adds[0][3]])
         put(-1, adds[1][:1])
-        put(0, [lambda: quantise_w(0), lambda: quantise_w(1), lambda: clear_w(0), lambda: clear_w(1)])
+        put(0, [quantise_w])
         for k in range(1, 4):
             put(bottom[1] - 7 + k, [adds[1][k]])
         for b in range(2, 4):

from contextlib import ExitStack

import concourse.mybir as mybir
from concourse.masks import make_identity

FP8X4 = mybir.dt.float8_e4m3fn_x4
BF16 = mybir.dt.bfloat16
F32 = mybir.dt.float32
U32 = mybir.dt.uint32
I32 = mybir.dt.int32
U8 = mybir.dt.uint8
ADD = mybir.AluOpType.add
MIN = mybir.AluOpType.min
MAX = mybir.AluOpType.max
ACT = mybir.ActivationFunctionType

P = 128
B = 4
HH = 64
WW = 64
PIX = HH * WW
NH = 512
NG = 4

PR, PC = 7, 18
STEP = PR - 2
COL0 = (0, 15, 31, 46)
SC = 16
UNITS = 5
NS = UNITS * STEP
XN_ROWS = 2 * NS + 3

V0 = 2 * NS
VR = HH - V0
VH = VR // 2
PITCH = 68

FLOPS = 2 * B * PIX * 1024 * P


def tile_qca_operator_deep_pa_t_kernel(tc, x_cat, w1, out):
    nc = tc.nc
    with ExitStack() as ctx:
        const = ctx.enter_context(tc.tile_pool(name="const", bufs=1))
        work = ctx.enter_context(tc.tile_pool(name="work", bufs=3))
        ees = ctx.enter_context(tc.tile_pool(name="ees", bufs=6))
        pairs = ctx.enter_context(tc.tile_pool(name="pairs", bufs=2))
        oos = ctx.enter_context(tc.tile_pool(name="oos", bufs=2))
        xpool = ctx.enter_context(tc.tile_pool(name="xpool", bufs=8))
        psum = ctx.enter_context(tc.psum_pool(name="psum", bufs=5))
        psn = ctx.enter_context(tc.psum_pool(name="psn", bufs=1))
        pst = ctx.enter_context(tc.psum_pool(name="pst", bufs=2))
        ctx.enter_context(tc.manual_schedule())

        x_all = const.tile([P, B, (HH + 3) * WW], BF16, name="x_all")
        x_sb = [x_all[:, b] for b in range(B)]

        def load(queue, b, r0, r1):
            queue.dma_start(
                out=x_sb[b][:, (r0 + 1) * WW : (r1 + 1) * WW],
                in_=x_cat[b].rearrange("c y x -> c (y x)")[:, r0 * WW : r1 * WW],
            )

        w_sb = const.tile([P, 1024], BF16, name="w_sb")
        load(nc.sync, 0, 0, 13)
        load(nc.scalar, 0, 24, 38)
        nc.scalar.dma_start(out=w_sb, in_=w1)
        load(nc.sync, 0, 38, HH)
        load(nc.sync, 0, 13, 24)
        for b in range(1, B):
            load(nc.sync, b, 0, HH)


        ident = const.tile([P, P], BF16, name="ident")
        make_identity(nc, ident)
        identf = const.tile([P, P], F32, name="identf")
        make_identity(nc, identf)
        nc.vector.memset(x_all[:, :, 0:WW], 0.0)
        idp = const.tile([P, PR + 2, PC + 2], BF16, name="idp")
        nc.vector.memset(idp, 0.0)
        permx = const.tile([P, P], BF16, name="permx")

        def permute(u, e):
            nc.vector.tensor_copy(
                out=permx[:, 64 * u + 32 * e : 64 * u + 32 * e + 32].rearrange("k (i a c) -> k i a c", i=4, a=4),
                in_=ident[:, 64 * e : 64 * e + 64].rearrange("k (a i c v) -> k v i a c", a=4, i=4, c=2)[:, u],
            )

        nv1 = const.tile([P, PR, PC + 2], BF16, name="nv1")
        nv2 = const.tile([P, PR, PC + 2], BF16, name="nv2")
        nh = const.tile([P, PR, PC], BF16, name="nh")
        nmat = const.tile([P, PR, PC], BF16, name="nmat")
        permute(0, 0)
        nc.vector.tensor_copy(
            out=idp[:, 1 : PR + 1, 1 : PC + 1], in_=ident[:, : PR * PC].rearrange("p (r c) -> p r c", c=PC)
        )
        permute(0, 1)
        nc.vector.tensor_tensor(out=nv1, in0=idp[:, 0:PR, :], in1=idp[:, 2 : PR + 2, :], op=ADD)
        permute(1, 0)
        nc.vector.tensor_tensor(out=nv2, in0=nv1, in1=idp[:, 1 : PR + 1, :], op=ADD)
        permute(1, 1)
        vcs = const.tile([P, 2, (VR + 1) * PITCH], F32, name="vcs")
        nbv = const.tile([P, B, (VR + 1) * WW], BF16, name="nbv")

        w_p = const.tile([P, 9, P], BF16, name="w_p")
        w_g = const.tile([P, NG, P, 4], BF16, name="w_g", align_bytes=64)
        w_codes = [const.tile([P, NG * P], U32, name="w_codes%d" % h, align_bytes=256) for h in range(2)]
        w_all = const.tile([P, NG * P], U32, name="w_all", align_bytes=256)
        w_scl = const.tile([P, NG * P], U8, name="w_scl", align_bytes=256)
        for h in range(2):
            nc.gpsimd.memset(w_codes[h], 0)

        def sort_w(e):
            nc.vector.tensor_copy(
                out=w_p[:, 0:8, 64 * e : 64 * e + 64].rearrange("o r (i a b) -> o r i a b", i=4, a=4),
                in_=w_sb[:, 512 * e : 512 * e + 512].rearrange("o (a i b r) -> o r i a b", a=4, i=4, b=4),
            )

        def w_stage_c(k):
            ps = pst.tile([P, 4, P], F32, name="xt_ps")
            for r in range(4):
                nc.tensor.transpose(
                    ps[:, r, :], w_p[:, 4 * k + r : 4 * k + r + 2].rearrange("p d c -> p (d c)").bitcast(F32), identf
                )
            words = w_g[:, 2 * k : 2 * k + 2].rearrange("p g o t -> p (g o t)").bitcast(F32)
            nc.scalar.copy(
                out=words.rearrange("p (g o u) -> p g o u", g=2, u=2), in_=ps.rearrange("p (g u) o -> p g o u", g=2, u=2)
            )

        def quantise_w():
            nc.vector.quantize_mx(
                out=w_all.bitcast(FP8X4), scales=w_scl, in_=w_g.rearrange("p g o t -> p (g o t)")
            )
            for h in range(2):
                part = slice(64 * h, 64 * h + 64)
                nc.sync.dma_start(out=w_codes[h][part, :].bitcast(I32), in_=w_all[part, :].bitcast(I32))

        strips = {}
        xts = {}

        def strips_of(b):
            if b not in strips:
                strips[b] = pairs.tile([P, 4, XN_ROWS * PC], BF16, name="strips")
            return strips[b]

        def strip_ops(b, r0, r1):
            q0, q1 = r0 + 1, r1 + 1

            def go(s):
                dst = strips_of(b).rearrange("p (a k) n -> p a k n", k=2)[:, :, s, q0 * PC : q1 * PC]
                src = x_sb[b][:, q0 * WW + COL0[s] : q1 * WW + COL0[s]].rearrange("p (y x) -> p y x", x=WW)[:, :, 0:62]
                nc.vector.tensor_copy(
                    out=dst.rearrange("p a (y x) -> p a y x", x=PC),
                    in_=src.rearrange("p y (a x) -> p a y x", a=2)[:, :, :, 0:PC],
                )

            return [lambda: go(0), lambda: go(1)]

        def transpose_unit(b, k):
            ps = pst.tile([P, 4, 2, 2, 64], BF16, name="xt_ps")
            for h in range(2):
                q0 = (NS * h + k * STEP) * PC
                for s in range(4):
                    nc.tensor.transpose(ps[:, s, :, h, :], strips[b][:, s, q0 : q0 + P], permx)
            return ps

        def copy_unit(b, k, ps):
            xt = xpool.tile([P, 4, 2, P], BF16, name="xt")
            nc.scalar.copy(out=xt.rearrange("p s u m -> p (s u m)"), in_=ps.rearrange("p s u h i -> p (s u h i)"))
            xts[b, k] = xt

        plan = [
            [(4, 0, 0), (4, 0, 0), (8, 0, 0), (8, 0, 0), (1, 7, 0)],
            [(8, 0, 2), (8, 0, 0), (4, 4, 2), (5, 3, 0)],
            [(8, 0, 2), (8, 0, 0), (4, 4, 2), (5, 3, 0)],
            [(8, 0, 2), (8, 0, 1), (4, 4, 2), (1, 3, 2), (4, 0, 0)],
        ]
        chunks = []
        relu = []
        for b in range(B):
            j, v = 0, 0
            for nj, nv, rl in plan[b]:
                chunks.append((b, j, j + nj, v, v + nv))
                relu.append(rl)
                j += nj
                v += nv
        nch = len(chunks)
        st = [dict() for c in chunks]
        first = [min(i for i in range(nch) if chunks[i][0] == b) for b in range(B)]
        bottom = [min(i for i in range(nch) if chunks[i][0] == b and chunks[i][4] > chunks[i][3]) for b in range(B)]

        def half(i):
            b, j0, j1, v0, v1 = chunks[i]
            return (j1 - j0 + v1 - v0) * WW

        def units_of(i):
            b, j0, j1, v0, v1 = chunks[i]
            return list(range(j0 // STEP, (j1 - 1) // STEP + 1)) if j1 > j0 else []

        vts = {}

        def rowsof(ap):
            return ap.rearrange("p (r c) -> p r c", c=WW)

        def add_ops(b):
            n = VR * WW
            flat = vcs[:, b % 2]
            up = x_sb[b][:, V0 * WW : V0 * WW + n]
            mid = x_sb[b][:, (V0 + 1) * WW : (V0 + 1) * WW + n]
            down = x_sb[b][:, (V0 + 2) * WW : (V0 + 2) * WW + n]
            tiles = {}

            def t(name):
                if name not in tiles:
                    tiles[name] = pairs.tile([P, VR * WW], F32, name=name)
                return tiles[name]

            def shifted(off):
                return flat[:, off : off + VR * PITCH].rearrange("p (r c) -> p r c", c=PITCH)[:, :, 0:WW]

            return [
                lambda: nc.vector.tensor_tensor(out=t("vo"), in0=up, in1=down, op=ADD),
                lambda: nc.vector.tensor_tensor(out=shifted(4), in0=rowsof(t("vo")), in1=rowsof(mid), op=ADD),
                lambda: nc.vector.tensor_tensor(out=rowsof(t("rr")), in0=shifted(3), in1=shifted(5), op=ADD),
                lambda: nc.vector.tensor_tensor(out=nbv[:, b, 0:n], in0=t("rr"), in1=t("vo"), op=ADD),
            ]

        def turn_bottom(b):
            ps = pst.tile([P, 4, 2, 2, 64], BF16, name="xt_ps")
            for h in range(2):
                for q in range(4):
                    a = (VH * h + 2 * q) * WW
                    nc.tensor.transpose(ps[:, q, :, h, :], nbv[:, b, a : a + P], permx)
            vt = xpool.tile([P, 4, 2, P], BF16, name="vt", bufs=2)
            nc.scalar.copy(out=vt.rearrange("p s u m -> p (s u m)"), in_=ps.rearrange("p s u h i -> p (s u h i)"))
            vts[b] = vt

        def sums(i):
            b, j0, j1, v0, v1 = chunks[i]
            nb = psn.tile([P, 2, NH], BF16, name="nb")
            st[i]["nb"] = nb
            for v in range(v0, v1, 2):
                for u in range(2):
                    c = (v - v0) * WW
                    nc.tensor.transpose(nb[:, u, c : c + P], vts[b][:, v // 2, u, :], ident)
            at_ = (v1 - v0) * WW
            for k in units_of(i):
                ra = max(j0, k * STEP)
                rb = min(j1, (k + 1) * STEP)
                for s in range(4):
                    c0 = SC * s - COL0[s]
                    for u in range(2):
                        to = nb[:, u, at_ + (ra - j0) * WW : at_ + (rb - j0) * WW].rearrange("p (y x) -> p y x", x=WW)
                        nc.tensor.matmul(
                            out=to[:, :, SC * s : SC * s + SC],
                            lhsT=xts[b, k][:, s, u, :],
                            rhs=nmat[:, ra - k * STEP + 1 : rb - k * STEP + 1, c0 : c0 + SC],
                            start=True,
                            stop=True,
                        )

        def repeat(i):
            n = half(i)
            rep = work.tile([P, 4 * NH], BF16, name="rep", align_bytes=256)
            st[i]["rep"] = rep
            nc.scalar.copy(
                out=rep[:, : 4 * n].rearrange("p (n r u) -> p n r u", r=2, u=2),
                in_=st[i]["nb"][:, :, :n].rearrange("p u n -> p n u").unsqueeze(2).to_broadcast([P, n, 2, 2]),
            )

        def quant_ops(i):
            n = half(i)
            codes = work.tile([P, NG, NH], U32, name="codes", align_bytes=256)
            scl = work.tile([P, NG, NH], U8, name="scl", align_bytes=256)
            st[i]["codes"] = codes
            st[i]["scl"] = scl
            rep = st[i]["rep"]

            def one(g):
                return lambda: nc.vector.quantize_mx(
                    out=codes[:, g, :n].bitcast(FP8X4), scales=scl[:, g, :n], in_=rep[:, : 4 * n]
                )

            return [one(g) for g in range(NG)]

        def multiply(i):
            codes = st[i]["codes"]
            scl = st[i]["scl"]
            n = half(i)
            accs = []
            for h in range(2):
                acc = psum.tile([P, NH], F32, name="acc")
                accs.append(acc)
            st[i]["accs"] = accs
            for g in range(NG):
                for h in range(2):
                    nc.tensor.matmul_mx(
                        out=accs[h][:, :n],
                        lhsT=w_codes[h][:, g * P : (g + 1) * P].bitcast(FP8X4),
                        lhsT_scale=w_scl[:, g * P : (g + 1) * P],
                        rhs=codes[:, g, :n].bitcast(FP8X4),
                        rhs_scale=scl[:, g, :n],
                        start=(g == 0),
                        stop=(g == NG - 1),
                    )

        def exps(i):
            n = half(i)
            ee = ees.tile([P, 2 * NH], F32, name="ee")
            st[i]["ee"] = ee
            if relu[i]:
                st[i]["oo"] = oos.tile([P, 2 * NH], F32, name="oo")
            for h in range(2):
                acc = st[i]["accs"][h][:, :n]
                nc.scalar.activation(out=ee[:, h * n : (h + 1) * n], in_=acc, func=ACT.Exp)
                if h < relu[i]:
                    nc.scalar.activation(out=st[i]["oo"][:, h * n : (h + 1) * n], in_=acc, func=ACT.Relu)

        def clamp_ops(i):
            n = half(i)
            ee = st[i]["ee"]
            if relu[i] == 2:
                return []
            a = relu[i] * n
            return [
                lambda: nc.vector.tensor_scalar(
                    out=ee[:, a : 2 * n], in0=ee[:, a : 2 * n], scalar1=1.0, scalar2=-1.0, op0=MIN, op1=ADD
                )
            ]

        def max_ops(i):
            ee = st[i]["ee"]
            n = half(i)
            ops = []
            if relu[i]:
                r = relu[i] * n
                ops.append(
                    lambda: nc.vector.scalar_tensor_tensor(
                        out=ee[:, :r], in0=ee[:, :r], scalar=-1.0, in1=st[i]["oo"][:, :r], op0=ADD, op1=MIN
                    )
                )
            for h in range(relu[i], 2):
                ops.append(
                    lambda h=h: nc.vector.tensor_tensor(
                        out=ee[:, h * n : (h + 1) * n], in0=ee[:, h * n : (h + 1) * n], in1=st[i]["accs"][h][:, :n], op=MAX
                    )
                )
            return ops

        def store(i):
            b, j0, j1, v0, v1 = chunks[i]
            ee = st[i]["ee"][:, : 2 * half(i)].rearrange("p (h n) -> p h n", h=2)
            nv = (v1 - v0) * WW
            if nv:
                to = out[b][:, V0:HH, :].rearrange("o (h y) x -> o h (y x)", h=2)
                nc.sync.dma_start(out=to[:, :, v0 * WW : v1 * WW], in_=ee[:, :, :nv])
            if j1 > j0:
                to = out[b][:, 0:V0, :].rearrange("o (h y) x -> o h (y x)", h=2)
                nc.sync.dma_start(out=to[:, :, j0 * WW : j1 * WW], in_=ee[:, :, nv:])

        extra = {}

        def put(i, ops):
            extra.setdefault(i, []).extend(ops)

        adds = [add_ops(b) for b in range(B)]
        for op in strip_ops(0, -1, 12) + strip_ops(0, 24, 37):
            op()
        nc.vector.memset(x_all[:, :, (HH + 1) * WW : (HH + 2) * WW], 0.0)
        nc.vector.tensor_tensor(out=nh, in0=nv2[:, :, 0:PC], in1=nv2[:, :, 2 : PC + 2], op=ADD)
        sort_w(0)
        nc.vector.tensor_tensor(out=nmat, in0=nh, in1=nv1[:, :, 1 : PC + 1], op=ADD)
        sort_w(1)
        nc.vector.memset(vcs.rearrange("p m (r c) -> p (m r) c", c=PITCH)[:, :, 0:4], 0.0)
        nc.vector.memset(nbv[:, :, VR * WW :], 0.0)
        nc.vector.tensor_copy(out=w_p[:, 8], in_=w_p[:, 0])
        s0 = strip_ops(0, 12, 24) + strip_ops(0, 37, 52)
        s1 = strip_ops(1, -1, XN_ROWS - 1)
        put(-3, [s0[0], s0[2], adds[0][0], s0[1], s0[3], adds[0][1]])
        put(-2, [s1[0], adds[0][2], s1[1], adds[0][3]])
        put(-1, adds[1][:1])
        put(0, [quantise_w])
        for k in range(1, 4):
            put(bottom[1] - 7 + k, [adds[1][k]])
        for b in range(2, 4):
            for k, op in enumerate(strip_ops(b, -1, XN_ROWS - 1)):
                put(first[b] - 5 + k, [op])
        for b in (2, 3):
            for k in range(4):
                put(bottom[b] - 7 + k * 1, [adds[b][k]])

        turn = {}
        for b in range(B):
            turn.setdefault(bottom[b] - 3, []).append(b)
        early = {-2: [lambda: w_stage_c(0), lambda: w_stage_c(1)]}

        def at(i, f):
            return f(i) if 0 <= i < nch else []

        def run(ops):
            for op in ops:
                op()

        done = set()

        def units_to_do(i):
            new = [(chunks[i][0], k) for k in units_of(i) if (chunks[i][0], k) not in done]
            done.update(new)
            return new

        for i in range(-3, nch + 3):
            q = at(i - 1, quant_ops)
            run(q[:2])
            run(at(i - 3, clamp_ops))
            run(q[2:])
            run(at(i - 3, max_ops))
            at(i - 3, store)
            at(i + 1, sums)
            at(i + 1, repeat)
            new = at(i + 3, units_to_do)
            for un in new[:1]:
                copy_unit(*un, transpose_unit(*un))
            for un in new[1:]:
                copy_unit(*un, transpose_unit(*un))
            for b in turn.get(i, []):
                turn_bottom(b)
            at(i - 1, multiply)
            at(i - 1, exps)
            run(early.get(i, []))
            run(extra.get(i, []))
